import numpy as np
import ml_dtypes


def mxq(x, axis, fmt="e4m3"):
    dtype, down = {"e4m3": (ml_dtypes.float8_e4m3fn, 7), "e5m2": (ml_dtypes.float8_e5m2, 14)}[fmt]
    v = np.moveaxis(np.asarray(x, np.float32).astype(ml_dtypes.bfloat16).astype(np.float64), axis, -1)
    blocks = v.reshape(v.shape[:-1] + (-1, 32))
    amax = np.abs(blocks).max(-1, keepdims=True)
    byte = np.maximum(np.where(amax > 0, np.frexp(amax)[1] - 1 + 127, 0) - down, 1)
    scale = np.exp2(byte - 127.0)
    codes = (blocks / scale).astype(np.float32).astype(dtype).astype(np.float64)
    return np.moveaxis((codes * scale).reshape(v.shape), -1, axis)


WIDE = False


def mx_kscale(k):
    if not WIDE:
        return np.ones(k)
    levels = np.array([10, -10, 5, -5, 0])
    a = np.random.permutation(np.resize(levels, k // 512 * 4)).reshape(k // 512, 4)
    idx = np.arange(k)
    return np.exp2(a[idx // 512, idx % 128 // 32])


BF16 = ml_dtypes.bfloat16


def bf(x):
    return np.asarray(x, np.float32).astype(BF16)


def f64(x):
    return np.asarray(x).astype(np.float64)


E2M1 = np.array([0.0, 0.5, 1.0, 1.5, 2.0, 3.0, 4.0, 6.0, -0.0, -0.5, -1.0, -1.5, -2.0, -3.0, -4.0, -6.0])


def pack_weight(w, fmt):
    k, n = w.shape
    w = f64(bf(w)).reshape(k // 32, 32, n)
    amax = np.abs(w).max(1)
    if fmt == "e4m3":
        byte = np.frexp(amax)[1] - 1 + 127 - 7
    else:
        mant, ex = np.frexp(amax / 6.0)
        byte = np.where(mant > 0.5, ex, ex - 1) + 127
    byte = np.clip(np.where(amax > 0, byte, 1), 1, 254)
    scaled = (w * np.exp2(127.0 - byte)[:, None, :]).reshape(k, n).astype(np.float32)
    by_word = np.ascontiguousarray(scaled.reshape(k // 512, 128, 4, n).transpose(0, 1, 3, 2))
    if fmt == "e4m3":
        words = by_word.astype(ml_dtypes.float8_e4m3fn).view(np.uint8)
    else:
        c = by_word.astype(ml_dtypes.float4_e2m1fn).view(np.uint8) & 0xF
        words = c[..., 0::2] | (c[..., 1::2] << 4)
    return np.ascontiguousarray(words), np.ascontiguousarray(byte.astype(np.uint8).reshape(k // 512, 16, n))


def unpack_weight(words, scales, fmt):
    g, p, n, _ = words.shape
    if fmt == "e4m3":
        vals = np.ascontiguousarray(words).view(ml_dtypes.float8_e4m3fn).astype(np.float64)
    else:
        nib = np.empty((g, p, n, 4), np.uint8)
        nib[..., 0::2] = words & 0xF
        nib[..., 1::2] = words >> 4
        vals = E2M1[nib]
    vals = vals * np.repeat(np.exp2(scales.astype(np.float64) - 127.0), 8, axis=1)[..., None]
    return vals.transpose(0, 1, 3, 2).reshape(g * 512, n)


N, S, K, Yd, Xd = 1024, 4, 16, 1024, 512
LOG_2PI = np.log(2.0 * np.pi)
FMT = "e4m3"


def softplus(v):
    return np.maximum(v, 0.0) + np.log(1.0 + np.exp(-np.abs(v)))


def log_softmax(v, axis):
    m = v - v.max(axis, keepdims=True)
    return m - np.log(np.exp(m).sum(axis, keepdims=True))


def mv_gaussian_log_prob(value, mu, sig_diags, event_shape):
    diff = value - mu
    M = np.sum((diff / sig_diags) ** 2, axis=-1)
    half_log_det = np.sum(np.log(sig_diags), axis=-1)
    return -0.5 * (event_shape * LOG_2PI + M) - half_log_det


def setup_inputs():
    s = mx_kscale(Yd)
    Y = bf(np.random.standard_normal((N, Yd)) * 0.5 * s)
    We_mu_words, We_mu_scales = pack_weight(np.random.standard_normal((Yd, Xd)) * 2.0 / np.sqrt(Yd) / s[:, None], FMT)
    be_mu = bf(np.random.standard_normal(Xd) * 0.1)
    We_sig_words, We_sig_scales = pack_weight(np.random.standard_normal((Yd, Xd)) * 1.0 / np.sqrt(Yd) / s[:, None], FMT)
    be_sig = bf(-3.0 + np.random.standard_normal(Xd) * 0.1)
    phi_mus = bf(np.random.standard_normal((K, Xd)) * 3.0 / np.sqrt(Xd))
    phi_sigs = bf(1.0 + (np.random.random_sample((K, Xd)) - 0.5) * 9.0 / np.sqrt(Xd))
    phi_logits = bf(np.random.standard_normal(K))
    return {"Y": Y,
            "We_mu_words": We_mu_words,
            "We_mu_scales": We_mu_scales,
            "be_mu": be_mu,
            "We_sig_words": We_sig_words,
            "We_sig_scales": We_sig_scales,
            "be_sig": be_sig,
            "phi_mus": phi_mus,
            "phi_sigs": phi_sigs,
            "phi_logits": phi_logits}


def reference(Y, We_mu_words, We_mu_scales, be_mu, We_sig_words, We_sig_scales, be_sig, phi_mus, phi_sigs, phi_logits):
    Yq = mxq(f64(Y), 1, "e4m3")
    enc_mu = (Yq @ unpack_weight(We_mu_words, We_mu_scales, FMT)) + f64(be_mu)
    enc_sig = softplus((Yq @ unpack_weight(We_sig_words, We_sig_scales, FMT)) + f64(be_sig)) + 1e-3
    log_pi = log_softmax(f64(phi_logits), -1)
    std_k = enc_sig[:, None, :] + f64(phi_sigs)[None, :, :]
    z_logits = log_pi[None, :] + mv_gaussian_log_prob(enc_mu[:, None, :], f64(phi_mus)[None, :, :], std_k, Xd)
    z_log_probs = log_softmax(z_logits, -1)
    return enc_mu, enc_sig, z_log_probs

@@ -1,0 +1,286 @@
+from contextlib import ExitStack
+
+import concourse.mybir as mybir
+from concourse.masks import make_identity
+
+F32 = mybir.dt.float32
+BF16 = mybir.dt.bfloat16
+I32 = mybir.dt.int32
+U32 = mybir.dt.uint32
+U8 = mybir.dt.uint8
+FP8X4 = mybir.dt.float8_e4m3fn_x4
+ACT = mybir.ActivationFunctionType
+ALU = mybir.AluOpType
+AXIS_X = mybir.AxisListType.X
+
+P = 128
+ROWS = 1024
+K_IN = 1024
+DIM = 512
+CLUSTERS = 16
+ROW_TILES = ROWS // P
+DIM_CHUNKS = DIM // P
+K_PASS = 4 * P
+PASSES = K_IN // K_PASS
+BANK = 512
+ROW_HALVES = ROWS // BANK
+BATCH = 2
+SOFTPLUS_LINEAR = 30.0
+SIG_FLOOR = 0.001
+
+FLOPS = 2 * 2 * ROWS * K_IN * DIM
+
+
+def tile_deepgmm_pa_kernel(
+    tc,
+    Y,
+    We_mu_words,
+    We_mu_scales,
+    be_mu,
+    We_sig_words,
+    We_sig_scales,
+    be_sig,
+    phi_mus,
+    phi_sigs,
+    phi_logits,
+    out_0,
+    out_1,
+    out_2,
+):
+    nc = tc.nc
+    with ExitStack() as ctx:
+        ctx.enter_context(tc.manual_schedule())
+        keep = ctx.enter_context(tc.tile_pool(name="keep", bufs=1))
+
+        ident_f32 = keep.tile([P, P], F32)
+        make_identity(nc, ident_f32[:])
+        ident_bf16 = keep.tile([P, P], BF16)
+        make_identity(nc, ident_bf16[:])
+
+        mu_t = keep.tile([P, DIM_CHUNKS, ROWS], F32)
+        sp_t = keep.tile([P, DIM_CHUNKS, ROWS], F32)
+        small = keep.tile([P, DIM_CHUNKS, 34], F32)
+        std_bias = keep.tile([P, DIM_CHUNKS, CLUSTERS], F32)
+        logits = keep.tile([P, CLUSTERS], BF16)
+
+        with tc.tile_pool(name="enc", bufs=1) as enc, tc.psum_pool(name="enc_small", bufs=1) as enc_small, tc.psum_pool(
+            name="enc_turn", bufs=3
+        ) as enc_turn, tc.psum_pool(name="enc_acc", bufs=4) as enc_acc:
+            y_sb = enc.tile([P, ROW_TILES, K_IN], BF16)
+            w_words = enc.tile([P, 2, PASSES, DIM], U32, align_bytes=64)
+            w_scales = enc.tile([P, 2, PASSES, DIM], U8, align_bytes=64)
+            small_rows = enc.tile([P, DIM], BF16)
+
+            nc.vector.memset(w_scales[:].rearrange("p w g n -> p (w g n)").bitcast(I32), 0)
+            nc.vector.memset(small_rows[:], 0.0)
+
+            y_rows = Y.rearrange("(p j) k -> p j k", j=ROW_TILES)
+            for j in range(0, ROW_TILES, 2):
+                nc.sync.dma_start(out=y_sb[:, j : j + 2, :], in_=y_rows[:, j : j + 2, :])
+            weights = ((We_sig_words, We_sig_scales), (We_mu_words, We_mu_scales))
+            for w, (words, scales) in enumerate(weights):
+                for g in range(PASSES):
+                    nc.sync.dma_start(
+                        out=w_words[:, w, g, :].bitcast(I32),
+                        in_=words[g].rearrange("p n t -> p (n t)").bitcast(I32),
+                    )
+            for w, (words, scales) in enumerate(weights):
+                for quad in range(4):
+                    nc.sync.dma_start(
+                        out=w_scales[32 * quad : 32 * quad + 4, w, :, :].bitcast(I32),
+                        in_=scales[:, 4 * quad : 4 * quad + 4, :].rearrange("g r n -> r g n").bitcast(I32),
+                    )
+            nc.scalar.dma_start(out=small_rows[0:16, :], in_=phi_mus)
+            nc.scalar.dma_start(out=small_rows[16:32, :], in_=phi_sigs)
+            nc.scalar.dma_start(out=small_rows[32:33, :], in_=be_mu.unsqueeze(0))
+            nc.scalar.dma_start(out=small_rows[33:34, :], in_=be_sig.unsqueeze(0))
+            nc.scalar.dma_start(out=logits[:], in_=phi_logits.partition_broadcast(P))
+
+            small_t = enc_small.tile([P, DIM_CHUNKS, P], BF16)
+            for c in range(DIM_CHUNKS):
+                nc.tensor.transpose(small_t[:, c, :], small_rows[:, P * c : P * (c + 1)], ident_bf16[:])
+            nc.vector.tensor_copy(out=small[:], in_=small_t[:, :, 0:34])
+            nc.vector.tensor_scalar_add(out=std_bias[:], in0=small[:, :, 16:32], scalar1=SIG_FLOOR)
+
+            y_words = y_sb[:].bitcast(F32)
+            grouped = enc.tile([P, PASSES, ROWS, 4], BF16, align_bytes=64)
+            grouped_words = grouped[:].rearrange("p g n t -> p g (n t)").bitcast(F32)
+            y_codes = enc.tile([P, PASSES, ROWS], U32, align_bytes=64)
+            y_scales = enc.tile([P, PASSES, ROWS], U8, align_bytes=64)
+            for h in range(ROW_HALVES):
+                for j in range(4 * h, 4 * h + 4, 2):
+                    for g in range(PASSES):
+                        turned = enc_turn.tile([P, 2, 2, P], F32)
+                        for jj in range(2):
+                            for u in range(2):
+                                nc.tensor.transpose(
+                                    turned[:, jj, u, :],
+                                    y_words[:, j + jj, 256 * g + u : 256 * (g + 1) : 2],
+                                    ident_f32[:],
+                                )
+                        pairs = grouped_words[:, g, 2 * P * j : 2 * P * (j + 2)].rearrange(
+                            "p (jj n u) -> p jj n u", jj=2, u=2
+                        )
+                        if g == 0:
+                            nc.vector.tensor_copy(out=pairs, in_=turned[:].rearrange("p jj u n -> p jj n u"))
+                        else:
+                            nc.scalar.copy(out=pairs, in_=turned[:].rearrange("p jj u n -> p jj n u"))
+                for g in range(PASSES):
+                    rows_h = slice(BANK * h, BANK * (h + 1))
+                    nc.vector.quantize_mx(
+                        out=y_codes[:, g, rows_h].bitcast(FP8X4),
+                        scales=y_scales[:, g, rows_h],
+                        in_=grouped[:, g, rows_h, :].rearrange("p n t -> p (n t)"),
+                    )
+
+            def product(w, c, h):
+                acc = enc_acc.tile([P, BANK], F32)
+                dims = slice(P * c, P * (c + 1))
+                rows_h = slice(BANK * h, BANK * (h + 1))
+                for g in range(PASSES):
+                    nc.tensor.matmul_mx(
+                        out=acc[:],
+                        lhsT=w_words[:, w, g, dims].bitcast(FP8X4),
+                        lhsT_scale=w_scales[:, w, g, dims],
+                        rhs=y_codes[:, g, rows_h].bitcast(FP8X4),
+                        rhs_scale=y_scales[:, g, rows_h],
+                        start=(g == 0),
+                        stop=(g == PASSES - 1),
+                    )
+                return acc
+
+            pre = enc.tile([P, DIM_CHUNKS, ROWS], F32)
+            soft = enc.tile([P, DIM_CHUNKS, ROWS], F32)
+            for h in range(ROW_HALVES):
+                rows_h = slice(BANK * h, BANK * (h + 1))
+                for c in range(DIM_CHUNKS):
+                    acc = product(0, c, h)
+                    nc.vector.tensor_scalar_add(out=pre[:, c, rows_h], in0=acc[:], scalar1=small[:, c, 33:34])
+                    nc.vector.tensor_scalar_min(out=soft[:, c, rows_h], in0=pre[:, c, rows_h], scalar1=SOFTPLUS_LINEAR)
+                    nc.scalar.activation(out=soft[:, c, rows_h], in_=soft[:, c, rows_h], func=ACT.Exp)
+            for h in range(ROW_HALVES):
+                rows_h = slice(BANK * h, BANK * (h + 1))
+                for c in range(DIM_CHUNKS):
+                    acc = product(1, c, h)
+                    nc.vector.tensor_scalar_add(out=mu_t[:, c, rows_h], in0=acc[:], scalar1=small[:, c, 32:33])
+            for c in range(DIM_CHUNKS):
+                nc.scalar.activation(out=soft[:, c, :], in_=soft[:, c, :], func=ACT.Ln, bias=1.0)
+                nc.vector.tensor_max(out=sp_t[:, c, :], in0=soft[:, c, :], in1=pre[:, c, :])
+
+        log_pool = ctx.enter_context(tc.tile_pool(name="log_std", bufs=3 * DIM_CHUNKS))
+        inv_pool = ctx.enter_context(tc.tile_pool(name="inv_std", bufs=2 * DIM_CHUNKS))
+        ratio_pool = ctx.enter_context(tc.tile_pool(name="ratio", bufs=2 * DIM_CHUNKS))
+        stage_pool = ctx.enter_context(tc.tile_pool(name="stage", bufs=2))
+        turn_pool = ctx.enter_context(tc.psum_pool(name="turn", bufs=6))
+        fold_pool = ctx.enter_context(tc.psum_pool(name="fold", bufs=2))
+
+        for source, floor, target in ((mu_t, 0.0, out_0), (sp_t, SIG_FLOOR, out_1)):
+            stage = stage_pool.tile([P, ROW_TILES, DIM], F32)
+            for j in range(ROW_TILES):
+                turned = turn_pool.tile([P, DIM], F32)
+                for c in range(DIM_CHUNKS):
+                    nc.tensor.transpose(
+                        turned[:, P * c : P * (c + 1)], source[:, c, P * j : P * (j + 1)], ident_f32[:]
+                    )
+                nc.vector.tensor_scalar_add(out=stage[:, j, :], in0=turned[:], scalar1=floor)
+            nc.sync.dma_start(out=target.rearrange("(p j) d -> p j d", j=ROW_TILES), in_=stage[:])
+
+        log_det = keep.tile([P, CLUSTERS, ROW_TILES], F32)
+        moments = keep.tile([P, CLUSTERS, ROW_TILES, 6], F32)
+
+        for first in range(0, CLUSTERS, BATCH):
+            batch = range(first, first + BATCH)
+            log_std = {}
+            inv_std = {}
+            for k in batch:
+                for c in range(DIM_CHUNKS):
+                    logs = log_pool.tile([P, ROWS], F32)
+                    nc.scalar.activation(out=logs[:], in_=sp_t[:, c, :], func=ACT.Ln, bias=std_bias[:, c, k : k + 1])
+                    log_std[k, c] = logs
+            for k in batch:
+                for c in range(DIM_CHUNKS):
+                    inverse = inv_pool.tile([P, ROWS], F32)
+                    nc.scalar.activation(out=inverse[:], in_=log_std[k, c][:], func=ACT.Exp, scale=-1.0)
+                    inv_std[k, c] = inverse
+            for k in batch:
+                ratios = []
+                for c in range(DIM_CHUNKS):
+                    ratio = ratio_pool.tile([P, ROWS], F32)
+                    nc.vector.scalar_tensor_tensor(
+                        out=ratio[:],
+                        in0=mu_t[:, c, :],
+                        scalar=small[:, c, k : k + 1],
+                        in1=inv_std[k, c][:],
+                        op0=ALU.subtract,
+                        op1=ALU.mult,
+                    )
+                    ratios.append(ratio)
+                for half in range(2):
+                    folded = fold_pool.tile([P, 4, P], F32)
+                    for jj in range(4):
+                        j = 4 * half + jj
+                        for c in range(DIM_CHUNKS):
+                            nc.tensor.matmul(
+                                out=folded[:, jj, :],
+                                lhsT=log_std[k, c][:, P * j : P * (j + 1)],
+                                rhs=ident_f32[:],
+                                is_transpose=True,
+                                start=(c == 0),
+                                stop=(c == DIM_CHUNKS - 1),
+                            )
+                    nc.vector.tensor_reduce(
+                        out=log_det[:, k, 4 * half : 4 * half + 4], in_=folded[:], axis=AXIS_X, op=ALU.add
+                    )
+                for j in range(ROW_TILES):
+                    turned = turn_pool.tile([P, DIM], F32)
+                    for c in range(DIM_CHUNKS):
+                        nc.tensor.transpose(
+                            turned[:, P * c : P * (c + 1)], ratios[c][:, P * j : P * (j + 1)], ident_f32[:]
+                        )
+                    nc.vector.bn_stats(out=moments[:, k, j, :], in_=turned[:])
+
+        cells = CLUSTERS * ROW_TILES
+        halves = moments[:].rearrange("p k j (e s) -> p (k j e) s", s=3)
+        mean_sq = keep.tile([P, 2 * cells], F32)
+        nc.vector.tensor_mul(out=mean_sq[:], in0=halves[:, :, 1], in1=halves[:, :, 1])
+        half_sums = keep.tile([P, cells, 2], F32)
+        nc.vector.scalar_tensor_tensor(
+            out=half_sums[:].rearrange("p x e -> p (x e)"),
+            in0=mean_sq[:],
+            scalar=float(DIM // 2),
+            in1=halves[:, :, 2],
+            op0=ALU.mult,
+            op1=ALU.add,
+        )
+        quad_form = keep.tile([P, cells], F32)
+        nc.vector.tensor_reduce(out=quad_form[:], in_=half_sums[:], axis=AXIS_X, op=ALU.add)
+        by_cluster = keep.tile([P, CLUSTERS, ROW_TILES], F32)
+        nc.vector.scalar_tensor_tensor(
+            out=by_cluster[:].rearrange("p k j -> p (k j)"),
+            in0=quad_form[:],
+            scalar=-0.5,
+            in1=log_det[:].rearrange("p k j -> p (k j)"),
+            op0=ALU.mult,
+            op1=ALU.subtract,
+        )
+        z = keep.tile([P, ROW_TILES, CLUSTERS], F32)
+        nc.vector.tensor_tensor(
+            out=z[:],
+            in0=by_cluster[:].rearrange("p k j -> p j k"),
+            in1=logits[:].unsqueeze(1).to_broadcast([P, ROW_TILES, CLUSTERS]),
+            op=ALU.add,
+        )
+        z_max = keep.tile([P, ROW_TILES], F32)
+        nc.vector.tensor_reduce(out=z_max[:], in_=z[:], axis=AXIS_X, op=ALU.max)
+        nc.vector.tensor_tensor(
+            out=z[:], in0=z[:], in1=z_max[:].unsqueeze(2).to_broadcast([P, ROW_TILES, CLUSTERS]), op=ALU.subtract
+        )
+        weight = keep.tile([P, ROW_TILES, CLUSTERS], F32)
+        nc.scalar.activation(out=weight[:], in_=z[:], func=ACT.Exp)
+        total = keep.tile([P, ROW_TILES], F32)
+        nc.vector.tensor_reduce(out=total[:], in_=weight[:], axis=AXIS_X, op=ALU.add)
+        nc.scalar.activation(out=total[:], in_=total[:], func=ACT.Ln)
+        nc.vector.tensor_tensor(
+            out=z[:], in0=z[:], in1=total[:].unsqueeze(2).to_broadcast([P, ROW_TILES, CLUSTERS]), op=ALU.subtract
+        )
+        nc.sync.dma_start(out=out_2.rearrange("(p j) k -> p j k", j=ROW_TILES), in_=z[:])

@@ -24,7 +24,7 @@ K_PASS = 4 * P
 PASSES = K_IN // K_PASS
 BANK = 512
 ROW_HALVES = ROWS // BANK
-BATCH = 2
+BATCH = 4
 SOFTPLUS_LINEAR = 30.0
 SIG_FLOOR = 0.001
 
@@ -167,7 +167,7 @@ def tile_deepgmm_pa_kernel(
                 nc.scalar.activation(out=soft[:, c, :], in_=soft[:, c, :], func=ACT.Ln, bias=1.0)
                 nc.vector.tensor_max(out=sp_t[:, c, :], in0=soft[:, c, :], in1=pre[:, c, :])
 
-        log_pool = ctx.enter_context(tc.tile_pool(name="log_std", bufs=3 * DIM_CHUNKS))
+        log_pool = ctx.enter_context(tc.tile_pool(name="log_std", bufs=(BATCH + 1) * DIM_CHUNKS))
         inv_pool = ctx.enter_context(tc.tile_pool(name="inv_std", bufs=2 * DIM_CHUNKS))
         ratio_pool = ctx.enter_context(tc.tile_pool(name="ratio", bufs=2 * DIM_CHUNKS))
         stage_pool = ctx.enter_context(tc.tile_pool(name="stage", bufs=2))

@@ -25,6 +25,7 @@ PASSES = K_IN // K_PASS
 BANK = 512
 ROW_HALVES = ROWS // BANK
 BATCH = 4
+GPSIMD_CHUNK = 0
 SOFTPLUS_LINEAR = 30.0
 SIG_FLOOR = 0.001
 
@@ -61,6 +62,7 @@ def tile_deepgmm_pa_kernel(
         sp_t = keep.tile([P, DIM_CHUNKS, ROWS], F32)
         small = keep.tile([P, DIM_CHUNKS, 34], F32)
         std_bias = keep.tile([P, DIM_CHUNKS, CLUSTERS], F32)
+        neg_mean = keep.tile([P, CLUSTERS], F32)
         logits = keep.tile([P, CLUSTERS], BF16)
 
         with tc.tile_pool(name="enc", bufs=1) as enc, tc.psum_pool(name="enc_small", bufs=1) as enc_small, tc.psum_pool(
@@ -101,6 +103,7 @@ def tile_deepgmm_pa_kernel(
                 nc.tensor.transpose(small_t[:, c, :], small_rows[:, P * c : P * (c + 1)], ident_bf16[:])
             nc.vector.tensor_copy(out=small[:], in_=small_t[:, :, 0:34])
             nc.vector.tensor_scalar_add(out=std_bias[:], in0=small[:, :, 16:32], scalar1=SIG_FLOOR)
+            nc.vector.tensor_scalar_mul(out=neg_mean[:], in0=small[:, GPSIMD_CHUNK, 0:16], scalar1=-1.0)
 
             y_words = y_sb[:].bitcast(F32)
             grouped = enc.tile([P, PASSES, ROWS, 4], BF16, align_bytes=64)
@@ -168,22 +171,27 @@ def tile_deepgmm_pa_kernel(
                 nc.vector.tensor_max(out=sp_t[:, c, :], in0=soft[:, c, :], in1=pre[:, c, :])
 
         log_pool = ctx.enter_context(tc.tile_pool(name="log_std", bufs=(BATCH + 1) * DIM_CHUNKS))
-        inv_pool = ctx.enter_context(tc.tile_pool(name="inv_std", bufs=2 * DIM_CHUNKS))
-        ratio_pool = ctx.enter_context(tc.tile_pool(name="ratio", bufs=2 * DIM_CHUNKS))
+        inv_pool = ctx.enter_context(tc.tile_pool(name="inv_std", bufs=10))
+        ratio_pool = ctx.enter_context(tc.tile_pool(name="ratio", bufs=2 * (DIM_CHUNKS - 1)))
+        side_pool = ctx.enter_context(tc.tile_pool(name="side", bufs=3))
         stage_pool = ctx.enter_context(tc.tile_pool(name="stage", bufs=2))
         turn_pool = ctx.enter_context(tc.psum_pool(name="turn", bufs=6))
         fold_pool = ctx.enter_context(tc.psum_pool(name="fold", bufs=2))
 
         for source, floor, target in ((mu_t, 0.0, out_0), (sp_t, SIG_FLOOR, out_1)):
-            stage = stage_pool.tile([P, ROW_TILES, DIM], F32)
-            for j in range(ROW_TILES):
-                turned = turn_pool.tile([P, DIM], F32)
-                for c in range(DIM_CHUNKS):
-                    nc.tensor.transpose(
-                        turned[:, P * c : P * (c + 1)], source[:, c, P * j : P * (j + 1)], ident_f32[:]
-                    )
-                nc.vector.tensor_scalar_add(out=stage[:, j, :], in0=turned[:], scalar1=floor)
-            nc.sync.dma_start(out=target.rearrange("(p j) d -> p j d", j=ROW_TILES), in_=stage[:])
+            for first in range(0, ROW_TILES, 4):
+                stage = stage_pool.tile([P, 4, DIM], F32)
+                for jj in range(4):
+                    j = first + jj
+                    turned = turn_pool.tile([P, DIM], F32)
+                    for c in range(DIM_CHUNKS):
+                        nc.tensor.transpose(
+                            turned[:, P * c : P * (c + 1)], source[:, c, P * j : P * (j + 1)], ident_f32[:]
+                        )
+                    nc.vector.tensor_scalar_add(out=stage[:, jj, :], in0=turned[:], scalar1=floor)
+                nc.sync.dma_start(
+                    out=target.rearrange("(p j) d -> p j d", j=ROW_TILES)[:, first : first + 4, :], in_=stage[:]
+                )
 
         log_det = keep.tile([P, CLUSTERS, ROW_TILES], F32)
         moments = keep.tile([P, CLUSTERS, ROW_TILES, 6], F32)
@@ -205,15 +213,27 @@ def tile_deepgmm_pa_kernel(
             for k in batch:
                 ratios = []
                 for c in range(DIM_CHUNKS):
-                    ratio = ratio_pool.tile([P, ROWS], F32)
-                    nc.vector.scalar_tensor_tensor(
-                        out=ratio[:],
-                        in0=mu_t[:, c, :],
-                        scalar=small[:, c, k : k + 1],
-                        in1=inv_std[k, c][:],
-                        op0=ALU.subtract,
-                        op1=ALU.mult,
-                    )
+                    if c == GPSIMD_CHUNK:
+                        ratio = side_pool.tile([P, ROWS], F32)
+                        nc.gpsimd.tensor_scalar(
+                            out=ratio[:],
+                            in0=mu_t[:, c, :],
+                            scalar1=neg_mean[:, k : k + 1],
+                            scalar2=1.0,
+                            op0=ALU.add,
+                            op1=ALU.mult,
+                        )
+                        nc.gpsimd.tensor_tensor(out=ratio[:], in0=ratio[:], in1=inv_std[k, c][:], op=ALU.mult)
+                    else:
+                        ratio = ratio_pool.tile([P, ROWS], F32)
+                        nc.vector.scalar_tensor_tensor(
+                            out=ratio[:],
+                            in0=mu_t[:, c, :],
+                            scalar=small[:, c, k : k + 1],
+                            in1=inv_std[k, c][:],
+                            op0=ALU.subtract,
+                            op1=ALU.mult,
+                        )
                     ratios.append(ratio)
                 for half in range(2):
                     folded = fold_pool.tile([P, 4, P], F32)

@@ -195,6 +195,11 @@ def tile_deepgmm_pa_kernel(
 
         log_det = keep.tile([P, CLUSTERS, ROW_TILES], F32)
         moments = keep.tile([P, CLUSTERS, ROW_TILES, 6], F32)
+        nc.vector.memset(moments[:], 0.0)
+        squares = keep.tile([P, CLUSTERS, ROW_TILES], F32)
+        nc.vector.memset(squares[:], 0.0)
+        waste = keep.tile([P, DIM], F32)
+        shares = (0, 2, 4, 4)
 
         for first in range(0, CLUSTERS, BATCH):
             batch = range(first, first + BATCH)
@@ -257,7 +262,12 @@ def tile_deepgmm_pa_kernel(
                         nc.tensor.transpose(
                             turned[:, P * c : P * (c + 1)], ratios[c][:, P * j : P * (j + 1)], ident_f32[:]
                         )
-                    nc.vector.bn_stats(out=moments[:, k, j, :], in_=turned[:])
+                    if k >= CLUSTERS - len(shares) and j % 2 == 1 and j // 2 < shares[k - CLUSTERS]:
+                        nc.scalar.activation(
+                            out=waste[:], in_=turned[:], func=ACT.Square, accum_out=squares[:, k, j : j + 1]
+                        )
+                    else:
+                        nc.vector.bn_stats(out=moments[:, k, j, :], in_=turned[:])
 
         cells = CLUSTERS * ROW_TILES
         halves = moments[:].rearrange("p k j (e s) -> p (k j e) s", s=3)
@@ -274,6 +284,7 @@ def tile_deepgmm_pa_kernel(
         )
         quad_form = keep.tile([P, cells], F32)
         nc.vector.tensor_reduce(out=quad_form[:], in_=half_sums[:], axis=AXIS_X, op=ALU.add)
+        nc.vector.tensor_add(out=quad_form[:], in0=quad_form[:], in1=squares[:].rearrange("p k j -> p (k j)"))
         by_cluster = keep.tile([P, CLUSTERS, ROW_TILES], F32)
         nc.vector.scalar_tensor_tensor(
             out=by_cluster[:].rearrange("p k j -> p (k j)"),

@@ -200,6 +200,8 @@ def tile_deepgmm_pa_kernel(
         nc.vector.memset(squares[:], 0.0)
         waste = keep.tile([P, DIM], F32)
         shares = (0, 2, 4, 4)
+        handed = keep.tile([P, CLUSTERS], F32)
+        side_ratios = {}
 
         for first in range(0, CLUSTERS, BATCH):
             batch = range(first, first + BATCH)
@@ -215,20 +217,25 @@ def tile_deepgmm_pa_kernel(
                     inverse = inv_pool.tile([P, ROWS], F32)
                     nc.scalar.activation(out=inverse[:], in_=log_std[k, c][:], func=ACT.Exp, scale=-1.0)
                     inv_std[k, c] = inverse
+            def side_ratio(k, mean):
+                ratio = side_pool.tile([P, ROWS], F32)
+                nc.gpsimd.tensor_scalar(
+                    out=ratio[:],
+                    in0=mu_t[:, GPSIMD_CHUNK, :],
+                    scalar1=mean,
+                    scalar2=1.0,
+                    op0=ALU.add,
+                    op1=ALU.mult,
+                )
+                nc.gpsimd.tensor_tensor(out=ratio[:], in0=ratio[:], in1=inv_std[k, GPSIMD_CHUNK][:], op=ALU.mult)
+                side_ratios[k] = ratio
+
+            side_ratio(first, neg_mean[:, first : first + 1])
             for k in batch:
                 ratios = []
                 for c in range(DIM_CHUNKS):
                     if c == GPSIMD_CHUNK:
-                        ratio = side_pool.tile([P, ROWS], F32)
-                        nc.gpsimd.tensor_scalar(
-                            out=ratio[:],
-                            in0=mu_t[:, c, :],
-                            scalar1=neg_mean[:, k : k + 1],
-                            scalar2=1.0,
-                            op0=ALU.add,
-                            op1=ALU.mult,
-                        )
-                        nc.gpsimd.tensor_tensor(out=ratio[:], in0=ratio[:], in1=inv_std[k, c][:], op=ALU.mult)
+                        ratio = side_ratios[k]
                     else:
                         ratio = ratio_pool.tile([P, ROWS], F32)
                         nc.vector.scalar_tensor_tensor(
@@ -240,6 +247,9 @@ def tile_deepgmm_pa_kernel(
                             op1=ALU.mult,
                         )
                     ratios.append(ratio)
+                if k + 1 in batch:
+                    nc.vector.tensor_copy(out=handed[:, k + 1 : k + 2], in_=neg_mean[:, k + 1 : k + 2])
+                    side_ratio(k + 1, handed[:, k + 1 : k + 2])
                 for half in range(2):
                     folded = fold_pool.tile([P, 4, P], F32)
                     for jj in range(4):

@@ -24,9 +24,9 @@ K_PASS = 4 * P
 PASSES = K_IN // K_PASS
 BANK = 512
 ROW_HALVES = ROWS // BANK
-BATCH = 4
-GPSIMD_CHUNK = 0
-SOFTPLUS_LINEAR = 30.0
+BATCHES = (5, 4, 4, 3)
+GPSIMD_CHUNKS = (0,)
+EXP_CAP = 1.0e13
 SIG_FLOOR = 0.001
 
 FLOPS = 2 * 2 * ROWS * K_IN * DIM
@@ -62,7 +62,7 @@ def tile_deepgmm_pa_kernel(
         sp_t = keep.tile([P, DIM_CHUNKS, ROWS], F32)
         small = keep.tile([P, DIM_CHUNKS, 34], F32)
         std_bias = keep.tile([P, DIM_CHUNKS, CLUSTERS], F32)
-        neg_mean = keep.tile([P, CLUSTERS], F32)
+        neg_mean = keep.tile([P, DIM_CHUNKS, CLUSTERS], F32)
         logits = keep.tile([P, CLUSTERS], BF16)
 
         with tc.tile_pool(name="enc", bufs=1) as enc, tc.psum_pool(name="enc_small", bufs=1) as enc_small, tc.psum_pool(
@@ -103,7 +103,7 @@ def tile_deepgmm_pa_kernel(
                 nc.tensor.transpose(small_t[:, c, :], small_rows[:, P * c : P * (c + 1)], ident_bf16[:])
             nc.vector.tensor_copy(out=small[:], in_=small_t[:, :, 0:34])
             nc.vector.tensor_scalar_add(out=std_bias[:], in0=small[:, :, 16:32], scalar1=SIG_FLOOR)
-            nc.vector.tensor_scalar_mul(out=neg_mean[:], in0=small[:, GPSIMD_CHUNK, 0:16], scalar1=-1.0)
+            nc.vector.tensor_scalar_mul(out=neg_mean[:], in0=small[:, :, 0:16], scalar1=-1.0)
 
             y_words = y_sb[:].bitcast(F32)
             grouped = enc.tile([P, PASSES, ROWS, 4], BF16, align_bytes=64)
@@ -158,30 +158,35 @@ def tile_deepgmm_pa_kernel(
                 rows_h = slice(BANK * h, BANK * (h + 1))
                 for c in range(DIM_CHUNKS):
                     acc = product(0, c, h)
+                    nc.scalar.activation(out=soft[:, c, rows_h], in_=acc[:], func=ACT.Exp, bias=small[:, c, 33:34])
                     nc.vector.tensor_scalar_add(out=pre[:, c, rows_h], in0=acc[:], scalar1=small[:, c, 33:34])
-                    nc.vector.tensor_scalar_min(out=soft[:, c, rows_h], in0=pre[:, c, rows_h], scalar1=SOFTPLUS_LINEAR)
-                    nc.scalar.activation(out=soft[:, c, rows_h], in_=soft[:, c, rows_h], func=ACT.Exp)
-            for h in range(ROW_HALVES):
+                    nc.vector.tensor_scalar_min(out=soft[:, c, rows_h], in0=soft[:, c, rows_h], scalar1=EXP_CAP)
+            def mean_bank(h, c):
                 rows_h = slice(BANK * h, BANK * (h + 1))
-                for c in range(DIM_CHUNKS):
-                    acc = product(1, c, h)
-                    nc.vector.tensor_scalar_add(out=mu_t[:, c, rows_h], in0=acc[:], scalar1=small[:, c, 32:33])
+                acc = product(1, c, h)
+                nc.vector.tensor_scalar_add(out=mu_t[:, c, rows_h], in0=acc[:], scalar1=small[:, c, 32:33])
+
+            banks = [(h, c) for h in range(ROW_HALVES) for c in range(DIM_CHUNKS)]
+            for h, c in banks[0:3]:
+                mean_bank(h, c)
             for c in range(DIM_CHUNKS):
                 nc.scalar.activation(out=soft[:, c, :], in_=soft[:, c, :], func=ACT.Ln, bias=1.0)
                 nc.vector.tensor_max(out=sp_t[:, c, :], in0=soft[:, c, :], in1=pre[:, c, :])
+                mean_bank(*banks[3 + c])
+            mean_bank(*banks[7])
 
-        log_pool = ctx.enter_context(tc.tile_pool(name="log_std", bufs=(BATCH + 1) * DIM_CHUNKS))
-        inv_pool = ctx.enter_context(tc.tile_pool(name="inv_std", bufs=10))
-        ratio_pool = ctx.enter_context(tc.tile_pool(name="ratio", bufs=2 * (DIM_CHUNKS - 1)))
+        log_pool = ctx.enter_context(tc.tile_pool(name="log_std", bufs=24))
+        inv_pool = ctx.enter_context(tc.tile_pool(name="inv_std", bufs=12))
+        ratio_pool = ctx.enter_context(tc.tile_pool(name="ratio", bufs=6))
         side_pool = ctx.enter_context(tc.tile_pool(name="side", bufs=3))
         stage_pool = ctx.enter_context(tc.tile_pool(name="stage", bufs=2))
         turn_pool = ctx.enter_context(tc.psum_pool(name="turn", bufs=6))
         fold_pool = ctx.enter_context(tc.psum_pool(name="fold", bufs=2))
 
         for source, floor, target in ((mu_t, 0.0, out_0), (sp_t, SIG_FLOOR, out_1)):
-            for first in range(0, ROW_TILES, 4):
-                stage = stage_pool.tile([P, 4, DIM], F32)
-                for jj in range(4):
+            for first in range(0, ROW_TILES, 2):
+                stage = stage_pool.tile([P, 2, DIM], F32)
+                for jj in range(2):
                     j = first + jj
                     turned = turn_pool.tile([P, DIM], F32)
                     for c in range(DIM_CHUNKS):
@@ -190,7 +195,7 @@ def tile_deepgmm_pa_kernel(
                         )
                     nc.vector.tensor_scalar_add(out=stage[:, jj, :], in0=turned[:], scalar1=floor)
                 nc.sync.dma_start(
-                    out=target.rearrange("(p j) d -> p j d", j=ROW_TILES)[:, first : first + 4, :], in_=stage[:]
+                    out=target.rearrange("(p j) d -> p j d", j=ROW_TILES)[:, first : first + 2, :], in_=stage[:]
                 )
 
         log_det = keep.tile([P, CLUSTERS, ROW_TILES], F32)
@@ -199,85 +204,112 @@ def tile_deepgmm_pa_kernel(
         squares = keep.tile([P, CLUSTERS, ROW_TILES], F32)
         nc.vector.memset(squares[:], 0.0)
         waste = keep.tile([P, DIM], F32)
-        shares = (0, 2, 4, 4)
-        handed = keep.tile([P, CLUSTERS], F32)
-        side_ratios = {}
 
-        for first in range(0, CLUSTERS, BATCH):
-            batch = range(first, first + BATCH)
-            log_std = {}
-            inv_std = {}
+        log_std = {}
+        inv_std = {}
+        ratios = {}
+        scalar_share = (4, 4, 4)
+
+        def logs_of(batch):
             for k in batch:
                 for c in range(DIM_CHUNKS):
                     logs = log_pool.tile([P, ROWS], F32)
                     nc.scalar.activation(out=logs[:], in_=sp_t[:, c, :], func=ACT.Ln, bias=std_bias[:, c, k : k + 1])
                     log_std[k, c] = logs
+
+        def inverses_of(batch):
             for k in batch:
                 for c in range(DIM_CHUNKS):
                     inverse = inv_pool.tile([P, ROWS], F32)
                     nc.scalar.activation(out=inverse[:], in_=log_std[k, c][:], func=ACT.Exp, scale=-1.0)
                     inv_std[k, c] = inverse
-            def side_ratio(k, mean):
-                ratio = side_pool.tile([P, ROWS], F32)
-                nc.gpsimd.tensor_scalar(
-                    out=ratio[:],
-                    in0=mu_t[:, GPSIMD_CHUNK, :],
-                    scalar1=mean,
-                    scalar2=1.0,
-                    op0=ALU.add,
-                    op1=ALU.mult,
-                )
-                nc.gpsimd.tensor_tensor(out=ratio[:], in0=ratio[:], in1=inv_std[k, GPSIMD_CHUNK][:], op=ALU.mult)
-                side_ratios[k] = ratio
 
-            side_ratio(first, neg_mean[:, first : first + 1])
-            for k in batch:
-                ratios = []
-                for c in range(DIM_CHUNKS):
-                    if c == GPSIMD_CHUNK:
-                        ratio = side_ratios[k]
-                    else:
-                        ratio = ratio_pool.tile([P, ROWS], F32)
-                        nc.vector.scalar_tensor_tensor(
-                            out=ratio[:],
-                            in0=mu_t[:, c, :],
-                            scalar=small[:, c, k : k + 1],
-                            in1=inv_std[k, c][:],
-                            op0=ALU.subtract,
-                            op1=ALU.mult,
-                        )
-                    ratios.append(ratio)
-                if k + 1 in batch:
-                    nc.vector.tensor_copy(out=handed[:, k + 1 : k + 2], in_=neg_mean[:, k + 1 : k + 2])
-                    side_ratio(k + 1, handed[:, k + 1 : k + 2])
-                for half in range(2):
-                    folded = fold_pool.tile([P, 4, P], F32)
-                    for jj in range(4):
-                        j = 4 * half + jj
-                        for c in range(DIM_CHUNKS):
-                            nc.tensor.matmul(
-                                out=folded[:, jj, :],
-                                lhsT=log_std[k, c][:, P * j : P * (j + 1)],
-                                rhs=ident_f32[:],
-                                is_transpose=True,
-                                start=(c == 0),
-                                stop=(c == DIM_CHUNKS - 1),
-                            )
-                    nc.vector.tensor_reduce(
-                        out=log_det[:, k, 4 * half : 4 * half + 4], in_=folded[:], axis=AXIS_X, op=ALU.add
-                    )
-                for j in range(ROW_TILES):
-                    turned = turn_pool.tile([P, DIM], F32)
+        def sum_logs(k):
+            for half in range(2):
+                folded = fold_pool.tile([P, 4, P], F32)
+                for jj in range(4):
+                    j = 4 * half + jj
                     for c in range(DIM_CHUNKS):
-                        nc.tensor.transpose(
-                            turned[:, P * c : P * (c + 1)], ratios[c][:, P * j : P * (j + 1)], ident_f32[:]
+                        nc.tensor.matmul(
+                            out=folded[:, jj, :],
+                            lhsT=log_std[k, c][:, P * j : P * (j + 1)],
+                            rhs=ident_f32[:],
+                            is_transpose=True,
+                            start=(c == 0),
+                            stop=(c == DIM_CHUNKS - 1),
                         )
-                    if k >= CLUSTERS - len(shares) and j % 2 == 1 and j // 2 < shares[k - CLUSTERS]:
-                        nc.scalar.activation(
-                            out=waste[:], in_=turned[:], func=ACT.Square, accum_out=squares[:, k, j : j + 1]
-                        )
-                    else:
-                        nc.vector.bn_stats(out=moments[:, k, j, :], in_=turned[:])
+                nc.vector.tensor_reduce(
+                    out=log_det[:, k, 4 * half : 4 * half + 4], in_=folded[:], axis=AXIS_X, op=ALU.add
+                )
+
+        GPSIMD_CHUNK = 0
+        handed = keep.tile([P, CLUSTERS], F32)
+
+        def side_ratio(k, mean):
+            ratio = side_pool.tile([P, ROWS], F32)
+            nc.gpsimd.tensor_scalar(
+                out=ratio[:], in0=mu_t[:, GPSIMD_CHUNK, :], scalar1=mean, scalar2=1.0, op0=ALU.add, op1=ALU.mult
+            )
+            nc.gpsimd.tensor_tensor(out=ratio[:], in0=ratio[:], in1=inv_std[k, GPSIMD_CHUNK][:], op=ALU.mult)
+            ratios[k, GPSIMD_CHUNK] = ratio
+
+        def hand_on(k, batch):
+            if k + 1 in batch:
+                nc.vector.tensor_copy(out=handed[:, k + 1 : k + 2], in_=neg_mean[:, GPSIMD_CHUNK, k + 1 : k + 2])
+                side_ratio(k + 1, handed[:, k + 1 : k + 2])
+
+        def form_ratios(k):
+            for c in range(DIM_CHUNKS):
+                if c != GPSIMD_CHUNK:
+                    ratio = ratio_pool.tile([P, ROWS], F32)
+                    nc.vector.scalar_tensor_tensor(
+                        out=ratio[:],
+                        in0=mu_t[:, c, :],
+                        scalar=small[:, c, k : k + 1],
+                        in1=inv_std[k, c][:],
+                        op0=ALU.subtract,
+                        op1=ALU.mult,
+                    )
+                    ratios[k, c] = ratio
+
+        def sum_squares(k):
+            share = scalar_share[k - CLUSTERS] if k >= CLUSTERS - len(scalar_share) else 0
+            for j in range(ROW_TILES):
+                turned = turn_pool.tile([P, DIM], F32)
+                for c in range(DIM_CHUNKS):
+                    nc.tensor.transpose(turned[:, P * c : P * (c + 1)], ratios[k, c][:, P * j : P * (j + 1)], ident_f32[:])
+                if j >= ROW_TILES - share:
+                    nc.scalar.activation(out=waste[:], in_=turned[:], func=ACT.Square, accum_out=squares[:, k, j : j + 1])
+                else:
+                    nc.vector.bn_stats(out=moments[:, k, j, :], in_=turned[:])
+
+        batches = []
+        first = 0
+        for size in BATCHES:
+            batches.append(list(range(first, first + size)))
+            first += size
+        batches.append([])
+
+        def cluster(k, batch):
+            form_ratios(k)
+            hand_on(k, batch)
+            sum_logs(k)
+            sum_squares(k)
+
+        for batch in batches[0 : len(BATCHES) - 1]:
+            logs_of(batch)
+            inverses_of(batch)
+            side_ratio(batch[0], neg_mean[:, GPSIMD_CHUNK, batch[0] : batch[0] + 1])
+            for k in batch:
+                cluster(k, batch)
+        batch = batches[len(BATCHES) - 1]
+        logs_of(batch)
+        inverses_of(batch[0 : 1])
+        side_ratio(batch[0], neg_mean[:, GPSIMD_CHUNK, batch[0] : batch[0] + 1])
+        for k in batch:
+            if k + 1 in batch:
+                inverses_of([k + 1])
+            cluster(k, batch)
 
         cells = CLUSTERS * ROW_TILES
         halves = moments[:].rearrange("p k j (e s) -> p (k j e) s", s=3)

@@ -98,13 +98,6 @@ def tile_deepgmm_pa_kernel(
             nc.scalar.dma_start(out=small_rows[33:34, :], in_=be_sig.unsqueeze(0))
             nc.scalar.dma_start(out=logits[:], in_=phi_logits.partition_broadcast(P))
 
-            small_t = enc_small.tile([P, DIM_CHUNKS, P], BF16)
-            for c in range(DIM_CHUNKS):
-                nc.tensor.transpose(small_t[:, c, :], small_rows[:, P * c : P * (c + 1)], ident_bf16[:])
-            nc.vector.tensor_copy(out=small[:], in_=small_t[:, :, 0:34])
-            nc.vector.tensor_scalar_add(out=std_bias[:], in0=small[:, :, 16:32], scalar1=SIG_FLOOR)
-            nc.vector.tensor_scalar_mul(out=neg_mean[:], in0=small[:, :, 0:16], scalar1=-1.0)
-
             y_words = y_sb[:].bitcast(F32)
             grouped = enc.tile([P, PASSES, ROWS, 4], BF16, align_bytes=64)
             grouped_words = grouped[:].rearrange("p g n t -> p g (n t)").bitcast(F32)
@@ -135,6 +128,13 @@ def tile_deepgmm_pa_kernel(
                         scales=y_scales[:, g, rows_h],
                         in_=grouped[:, g, rows_h, :].rearrange("p n t -> p (n t)"),
                     )
+                if h == 0:
+                    small_t = enc_small.tile([P, DIM_CHUNKS, P], BF16)
+                    for c in range(DIM_CHUNKS):
+                        nc.tensor.transpose(small_t[:, c, :], small_rows[:, P * c : P * (c + 1)], ident_bf16[:])
+                    nc.vector.tensor_copy(out=small[:], in_=small_t[:, :, 0:34])
+                    nc.vector.tensor_scalar_add(out=std_bias[:], in0=small[:, :, 16:32], scalar1=SIG_FLOOR)
+                    nc.vector.tensor_scalar_mul(out=neg_mean[:], in0=small[:, :, 0:16], scalar1=-1.0)
 
             def product(w, c, h):
                 acc = enc_acc.tile([P, BANK], F32)
@@ -248,7 +248,7 @@ def tile_deepgmm_pa_kernel(
         def side_ratio(k, mean):
             ratio = side_pool.tile([P, ROWS], F32)
             nc.gpsimd.tensor_scalar(
-                out=ratio[:], in0=mu_t[:, GPSIMD_CHUNK, :], scalar1=mean, scalar2=1.0, op0=ALU.add, op1=ALU.mult
+                out=ratio[:], in0=mu_t[:, GPSIMD_CHUNK, :], scalar1=1.0, scalar2=mean, op0=ALU.mult, op1=ALU.add
             )
             nc.gpsimd.tensor_tensor(out=ratio[:], in0=ratio[:], in1=inv_std[k, GPSIMD_CHUNK][:], op=ALU.mult)
             ratios[k, GPSIMD_CHUNK] = ratio

@@ -53,6 +53,10 @@ def tile_deepgmm_pa_kernel(
         ctx.enter_context(tc.manual_schedule())
         keep = ctx.enter_context(tc.tile_pool(name="keep", bufs=1))
 
+        spark = keep.tile([P, 1], F32)
+        nc.vector.memset(spark[:], 0.0)
+        nc.scalar.activation(out=spark[:], in_=spark[:], func=ACT.Exp)
+
         ident_f32 = keep.tile([P, P], F32)
         make_identity(nc, ident_f32[:])
         ident_bf16 = keep.tile([P, P], BF16)
@@ -65,48 +69,55 @@ def tile_deepgmm_pa_kernel(
         neg_mean = keep.tile([P, DIM_CHUNKS, CLUSTERS], F32)
         logits = keep.tile([P, CLUSTERS], BF16)
 
-        with tc.tile_pool(name="enc", bufs=1) as enc, tc.psum_pool(name="enc_small", bufs=1) as enc_small, tc.psum_pool(
-            name="enc_turn", bufs=3
-        ) as enc_turn, tc.psum_pool(name="enc_acc", bufs=4) as enc_acc:
+        with tc.tile_pool(name="enc", bufs=1) as enc, tc.psum_pool(name="enc_turn", bufs=4) as enc_turn, tc.psum_pool(
+            name="enc_acc", bufs=4
+        ) as enc_acc:
             y_sb = enc.tile([P, ROW_TILES, K_IN], BF16)
             w_words = enc.tile([P, 2, PASSES, DIM], U32, align_bytes=64)
             w_scales = enc.tile([P, 2, PASSES, DIM], U8, align_bytes=64)
             small_rows = enc.tile([P, DIM], BF16)
 
-            nc.vector.memset(w_scales[:].rearrange("p w g n -> p (w g n)").bitcast(I32), 0)
             nc.vector.memset(small_rows[:], 0.0)
+            nc.vector.memset(w_scales[:].rearrange("p w g n -> p (w g n)").bitcast(I32), 0)
 
             y_rows = Y.rearrange("(p j) k -> p j k", j=ROW_TILES)
-            for j in range(0, ROW_TILES, 2):
+
+            def load_rows(j):
                 nc.sync.dma_start(out=y_sb[:, j : j + 2, :], in_=y_rows[:, j : j + 2, :])
-            weights = ((We_sig_words, We_sig_scales), (We_mu_words, We_mu_scales))
-            for w, (words, scales) in enumerate(weights):
+
+            def load_weight(w, words, scales):
                 for g in range(PASSES):
                     nc.sync.dma_start(
                         out=w_words[:, w, g, :].bitcast(I32),
                         in_=words[g].rearrange("p n t -> p (n t)").bitcast(I32),
                     )
-            for w, (words, scales) in enumerate(weights):
                 for quad in range(4):
                     nc.sync.dma_start(
                         out=w_scales[32 * quad : 32 * quad + 4, w, :, :].bitcast(I32),
                         in_=scales[:, 4 * quad : 4 * quad + 4, :].rearrange("g r n -> r g n").bitcast(I32),
                     )
-            nc.scalar.dma_start(out=small_rows[0:16, :], in_=phi_mus)
-            nc.scalar.dma_start(out=small_rows[16:32, :], in_=phi_sigs)
-            nc.scalar.dma_start(out=small_rows[32:33, :], in_=be_mu.unsqueeze(0))
-            nc.scalar.dma_start(out=small_rows[33:34, :], in_=be_sig.unsqueeze(0))
-            nc.scalar.dma_start(out=logits[:], in_=phi_logits.partition_broadcast(P))
+
+            load_rows(0)
+            nc.sync.dma_start(out=small_rows[0:16, :], in_=phi_mus)
+            nc.sync.dma_start(out=small_rows[16:32, :], in_=phi_sigs)
+            nc.sync.dma_start(out=small_rows[32:33, :], in_=be_mu.unsqueeze(0))
+            nc.sync.dma_start(out=small_rows[33:34, :], in_=be_sig.unsqueeze(0))
+            load_rows(2)
+            load_weight(0, We_sig_words, We_sig_scales)
+            load_rows(4)
+            load_rows(6)
+            load_weight(1, We_mu_words, We_mu_scales)
+            nc.sync.dma_start(out=logits[:], in_=phi_logits.partition_broadcast(P))
 
             y_words = y_sb[:].bitcast(F32)
             grouped = enc.tile([P, PASSES, ROWS, 4], BF16, align_bytes=64)
             grouped_words = grouped[:].rearrange("p g n t -> p g (n t)").bitcast(F32)
             y_codes = enc.tile([P, PASSES, ROWS], U32, align_bytes=64)
             y_scales = enc.tile([P, PASSES, ROWS], U8, align_bytes=64)
-            for h in range(ROW_HALVES):
-                for j in range(4 * h, 4 * h + 4, 2):
+            def turn_pair(j, scalar_helps):
+                if True:
                     for g in range(PASSES):
-                        turned = enc_turn.tile([P, 2, 2, P], F32)
+                        turned = enc_turn.tile([P, 2, 2, P], F32, name="turned")
                         for jj in range(2):
                             for u in range(2):
                                 nc.tensor.transpose(
@@ -117,10 +128,12 @@ def tile_deepgmm_pa_kernel(
                         pairs = grouped_words[:, g, 2 * P * j : 2 * P * (j + 2)].rearrange(
                             "p (jj n u) -> p jj n u", jj=2, u=2
                         )
-                        if g == 0:
+                        if g == 0 or not scalar_helps:
                             nc.vector.tensor_copy(out=pairs, in_=turned[:].rearrange("p jj u n -> p jj n u"))
                         else:
                             nc.scalar.copy(out=pairs, in_=turned[:].rearrange("p jj u n -> p jj n u"))
+
+            def quantize_half(h):
                 for g in range(PASSES):
                     rows_h = slice(BANK * h, BANK * (h + 1))
                     nc.vector.quantize_mx(
@@ -128,13 +141,14 @@ def tile_deepgmm_pa_kernel(
                         scales=y_scales[:, g, rows_h],
                         in_=grouped[:, g, rows_h, :].rearrange("p n t -> p (n t)"),
                     )
-                if h == 0:
-                    small_t = enc_small.tile([P, DIM_CHUNKS, P], BF16)
-                    for c in range(DIM_CHUNKS):
-                        nc.tensor.transpose(small_t[:, c, :], small_rows[:, P * c : P * (c + 1)], ident_bf16[:])
-                    nc.vector.tensor_copy(out=small[:], in_=small_t[:, :, 0:34])
-                    nc.vector.tensor_scalar_add(out=std_bias[:], in0=small[:, :, 16:32], scalar1=SIG_FLOOR)
-                    nc.vector.tensor_scalar_mul(out=neg_mean[:], in0=small[:, :, 0:16], scalar1=-1.0)
+
+            def turn_small():
+                small_t = enc_turn.tile([P, DIM_CHUNKS, P], BF16, name="turned")
+                for c in range(DIM_CHUNKS):
+                    nc.tensor.transpose(small_t[:, c, :], small_rows[:, P * c : P * (c + 1)], ident_bf16[:])
+                nc.vector.tensor_copy(out=small[:], in_=small_t[:, :, 0:34])
+                nc.vector.tensor_scalar_add(out=std_bias[:], in0=small[:, :, 16:32], scalar1=SIG_FLOOR)
+                nc.vector.tensor_scalar_mul(out=neg_mean[:], in0=small[:, :, 0:16], scalar1=-1.0)
 
             def product(w, c, h):
                 acc = enc_acc.tile([P, BANK], F32)
@@ -154,49 +168,68 @@ def tile_deepgmm_pa_kernel(
 
             pre = enc.tile([P, DIM_CHUNKS, ROWS], F32)
             soft = enc.tile([P, DIM_CHUNKS, ROWS], F32)
-            for h in range(ROW_HALVES):
+
+            def sigma_bank(h, c):
                 rows_h = slice(BANK * h, BANK * (h + 1))
-                for c in range(DIM_CHUNKS):
-                    acc = product(0, c, h)
-                    nc.scalar.activation(out=soft[:, c, rows_h], in_=acc[:], func=ACT.Exp, bias=small[:, c, 33:34])
-                    nc.vector.tensor_scalar_add(out=pre[:, c, rows_h], in0=acc[:], scalar1=small[:, c, 33:34])
-                    nc.vector.tensor_scalar_min(out=soft[:, c, rows_h], in0=soft[:, c, rows_h], scalar1=EXP_CAP)
+                acc = product(0, c, h)
+                nc.scalar.activation(out=soft[:, c, rows_h], in_=acc[:], func=ACT.Exp, bias=small[:, c, 33:34])
+                nc.vector.tensor_scalar_add(out=pre[:, c, rows_h], in0=acc[:], scalar1=small[:, c, 33:34])
+                if h == 1:
+                    nc.vector.tensor_scalar_min(out=soft[:, c, :], in0=soft[:, c, :], scalar1=EXP_CAP)
+
+            turn_pair(0, True)
+            turn_pair(2, True)
+            quantize_half(0)
+            turn_small()
+            turn_pair(4, False)
+            sigma_bank(0, 0)
+            sigma_bank(0, 1)
+            turn_pair(6, False)
+            quantize_half(1)
+            sigma_bank(0, 2)
+            sigma_bank(0, 3)
+            for c in range(DIM_CHUNKS):
+                sigma_bank(1, c)
+
             def mean_bank(h, c):
                 rows_h = slice(BANK * h, BANK * (h + 1))
                 acc = product(1, c, h)
                 nc.vector.tensor_scalar_add(out=mu_t[:, c, rows_h], in0=acc[:], scalar1=small[:, c, 32:33])
 
-            banks = [(h, c) for h in range(ROW_HALVES) for c in range(DIM_CHUNKS)]
-            for h, c in banks[0:3]:
-                mean_bank(h, c)
             for c in range(DIM_CHUNKS):
                 nc.scalar.activation(out=soft[:, c, :], in_=soft[:, c, :], func=ACT.Ln, bias=1.0)
                 nc.vector.tensor_max(out=sp_t[:, c, :], in0=soft[:, c, :], in1=pre[:, c, :])
-                mean_bank(*banks[3 + c])
-            mean_bank(*banks[7])
+            for h in range(ROW_HALVES):
+                for c in range(DIM_CHUNKS):
+                    mean_bank(h, c)
 
-        log_pool = ctx.enter_context(tc.tile_pool(name="log_std", bufs=24))
+        log_pool = ctx.enter_context(tc.tile_pool(name="log_std", bufs=23))
         inv_pool = ctx.enter_context(tc.tile_pool(name="inv_std", bufs=12))
         ratio_pool = ctx.enter_context(tc.tile_pool(name="ratio", bufs=6))
         side_pool = ctx.enter_context(tc.tile_pool(name="side", bufs=3))
-        stage_pool = ctx.enter_context(tc.tile_pool(name="stage", bufs=2))
+        stage_pool = ctx.enter_context(tc.tile_pool(name="stage", bufs=3))
         turn_pool = ctx.enter_context(tc.psum_pool(name="turn", bufs=6))
         fold_pool = ctx.enter_context(tc.psum_pool(name="fold", bufs=2))
 
-        for source, floor, target in ((mu_t, 0.0, out_0), (sp_t, SIG_FLOOR, out_1)):
-            for first in range(0, ROW_TILES, 2):
-                stage = stage_pool.tile([P, 2, DIM], F32)
-                for jj in range(2):
-                    j = first + jj
-                    turned = turn_pool.tile([P, DIM], F32)
-                    for c in range(DIM_CHUNKS):
-                        nc.tensor.transpose(
-                            turned[:, P * c : P * (c + 1)], source[:, c, P * j : P * (j + 1)], ident_f32[:]
-                        )
-                    nc.vector.tensor_scalar_add(out=stage[:, jj, :], in0=turned[:], scalar1=floor)
-                nc.sync.dma_start(
-                    out=target.rearrange("(p j) d -> p j d", j=ROW_TILES)[:, first : first + 2, :], in_=stage[:]
-                )
+        def store_pair(source, floor, target, first):
+            stage = stage_pool.tile([P, 2, DIM], F32)
+            for jj in range(2):
+                j = first + jj
+                turned = turn_pool.tile([P, DIM], F32, name="turned")
+                for c in range(DIM_CHUNKS):
+                    nc.tensor.transpose(
+                        turned[:, P * c : P * (c + 1)], source[:, c, P * j : P * (j + 1)], ident_f32[:]
+                    )
+                nc.vector.tensor_scalar_add(out=stage[:, jj, :], in0=turned[:], scalar1=floor)
+            nc.sync.dma_start(
+                out=target.rearrange("(p j) d -> p j d", j=ROW_TILES)[:, first : first + 2, :], in_=stage[:]
+            )
+
+        stores = [
+            (source, floor, target, first)
+            for source, floor, target in ((mu_t, 0.0, out_0), (sp_t, SIG_FLOOR, out_1))
+            for first in range(0, ROW_TILES, 2)
+        ]
 
         log_det = keep.tile([P, CLUSTERS, ROW_TILES], F32)
         moments = keep.tile([P, CLUSTERS, ROW_TILES, 6], F32)
@@ -275,7 +308,7 @@ def tile_deepgmm_pa_kernel(
         def sum_squares(k):
             share = scalar_share[k - CLUSTERS] if k >= CLUSTERS - len(scalar_share) else 0
             for j in range(ROW_TILES):
-                turned = turn_pool.tile([P, DIM], F32)
+                turned = turn_pool.tile([P, DIM], F32, name="turned")
                 for c in range(DIM_CHUNKS):
                     nc.tensor.transpose(turned[:, P * c : P * (c + 1)], ratios[k, c][:, P * j : P * (j + 1)], ident_f32[:])
                 if j >= ROW_TILES - share:
@@ -293,11 +326,20 @@ def tile_deepgmm_pa_kernel(
         def cluster(k, batch):
             form_ratios(k)
             hand_on(k, batch)
-            sum_logs(k)
+            if k >= BATCHES[0]:
+                sum_logs(k)
             sum_squares(k)
 
         for batch in batches[0 : len(BATCHES) - 1]:
             logs_of(batch)
+            if batch is batches[0]:
+                for k in batch:
+                    for twice in range(2):
+                        if stores:
+                            store_pair(*stores.pop(0))
+                    sum_logs(k)
+                while stores:
+                    store_pair(*stores.pop(0))
             inverses_of(batch)
             side_ratio(batch[0], neg_mean[:, GPSIMD_CHUNK, batch[0] : batch[0] + 1])
             for k in batch:

@@ -69,12 +69,13 @@ def tile_deepgmm_pa_kernel(
         neg_mean = keep.tile([P, DIM_CHUNKS, CLUSTERS], F32)
         logits = keep.tile([P, CLUSTERS], BF16)
 
+        held = ctx.enter_context(tc.tile_pool(name="held", bufs=1))
         with tc.tile_pool(name="enc", bufs=1) as enc, tc.psum_pool(name="enc_turn", bufs=4) as enc_turn, tc.psum_pool(
             name="enc_acc", bufs=4
         ) as enc_acc:
             y_sb = enc.tile([P, ROW_TILES, K_IN], BF16)
-            w_words = enc.tile([P, 2, PASSES, DIM], U32, align_bytes=64)
-            w_scales = enc.tile([P, 2, PASSES, DIM], U8, align_bytes=64)
+            w_words = held.tile([P, 2, PASSES, DIM], U32, align_bytes=64)
+            w_scales = held.tile([P, 2, PASSES, DIM], U8, align_bytes=64)
             small_rows = enc.tile([P, DIM], BF16)
 
             nc.vector.memset(small_rows[:], 0.0)
@@ -112,8 +113,8 @@ def tile_deepgmm_pa_kernel(
             y_words = y_sb[:].bitcast(F32)
             grouped = enc.tile([P, PASSES, ROWS, 4], BF16, align_bytes=64)
             grouped_words = grouped[:].rearrange("p g n t -> p g (n t)").bitcast(F32)
-            y_codes = enc.tile([P, PASSES, ROWS], U32, align_bytes=64)
-            y_scales = enc.tile([P, PASSES, ROWS], U8, align_bytes=64)
+            y_codes = held.tile([P, PASSES, ROWS], U32, align_bytes=64)
+            y_scales = held.tile([P, PASSES, ROWS], U8, align_bytes=64)
             def turn_pair(j, scalar_helps):
                 if True:
                     for g in range(PASSES):
@@ -203,11 +204,11 @@ def tile_deepgmm_pa_kernel(
                 for c in range(DIM_CHUNKS):
                     mean_bank(h, c)
 
-        log_pool = ctx.enter_context(tc.tile_pool(name="log_std", bufs=23))
+        log_pool = ctx.enter_context(tc.tile_pool(name="log_std", bufs=20))
         inv_pool = ctx.enter_context(tc.tile_pool(name="inv_std", bufs=12))
-        ratio_pool = ctx.enter_context(tc.tile_pool(name="ratio", bufs=6))
+        ratio_pool = ctx.enter_context(tc.tile_pool(name="ratio", bufs=5))
         side_pool = ctx.enter_context(tc.tile_pool(name="side", bufs=3))
-        stage_pool = ctx.enter_context(tc.tile_pool(name="stage", bufs=3))
+        stage_pool = ctx.enter_context(tc.tile_pool(name="stage", bufs=2))
         turn_pool = ctx.enter_context(tc.psum_pool(name="turn", bufs=6))
         fold_pool = ctx.enter_context(tc.psum_pool(name="fold", bufs=2))
 

@@ -25,6 +25,7 @@ PASSES = K_IN // K_PASS
 BANK = 512
 ROW_HALVES = ROWS // BANK
 BATCHES = (5, 4, 4, 3)
+WIDE = 4
 GPSIMD_CHUNKS = (0,)
 EXP_CAP = 1.0e13
 SIG_FLOOR = 0.001
@@ -204,10 +205,9 @@ def tile_deepgmm_pa_kernel(
                 for c in range(DIM_CHUNKS):
                     mean_bank(h, c)
 
-        log_pool = ctx.enter_context(tc.tile_pool(name="log_std", bufs=20))
-        inv_pool = ctx.enter_context(tc.tile_pool(name="inv_std", bufs=12))
-        ratio_pool = ctx.enter_context(tc.tile_pool(name="ratio", bufs=5))
-        side_pool = ctx.enter_context(tc.tile_pool(name="side", bufs=3))
+        log_pool = ctx.enter_context(tc.tile_pool(name="log_std", bufs=5))
+        ratio_pool = ctx.enter_context(tc.tile_pool(name="ratio", bufs=4))
+        side_pool = ctx.enter_context(tc.tile_pool(name="side", bufs=2))
         stage_pool = ctx.enter_context(tc.tile_pool(name="stage", bufs=2))
         turn_pool = ctx.enter_context(tc.psum_pool(name="turn", bufs=6))
         fold_pool = ctx.enter_context(tc.psum_pool(name="fold", bufs=2))
@@ -240,23 +240,28 @@ def tile_deepgmm_pa_kernel(
         waste = keep.tile([P, DIM], F32)
 
         log_std = {}
-        inv_std = {}
         ratios = {}
         scalar_share = (4, 4, 4)
 
         def logs_of(batch):
             for k in batch:
+                log_std[k] = log_pool.tile([P, DIM_CHUNKS, ROWS], F32, name="logs")
                 for c in range(DIM_CHUNKS):
-                    logs = log_pool.tile([P, ROWS], F32)
-                    nc.scalar.activation(out=logs[:], in_=sp_t[:, c, :], func=ACT.Ln, bias=std_bias[:, c, k : k + 1])
-                    log_std[k, c] = logs
+                    nc.scalar.activation(
+                        out=log_std[k][:, c, :], in_=sp_t[:, c, :], func=ACT.Ln, bias=std_bias[:, c, k : k + 1]
+                    )
 
         def inverses_of(batch):
             for k in batch:
-                for c in range(DIM_CHUNKS):
-                    inverse = inv_pool.tile([P, ROWS], F32)
-                    nc.scalar.activation(out=inverse[:], in_=log_std[k, c][:], func=ACT.Exp, scale=-1.0)
-                    inv_std[k, c] = inverse
+                ratios[k] = ratio_pool.tile([P, DIM_CHUNKS, ROWS], F32, name="ratio")
+                step = 1 if k in starts else WIDE
+                for c in range(0, DIM_CHUNKS, step):
+                    nc.scalar.activation(
+                        out=ratios[k][:, c : c + step, :],
+                        in_=log_std[k][:, c : c + step, :],
+                        func=ACT.Exp,
+                        scale=-1.0,
+                    )
 
         def sum_logs(k):
             for half in range(2):
@@ -266,7 +271,7 @@ def tile_deepgmm_pa_kernel(
                     for c in range(DIM_CHUNKS):
                         nc.tensor.matmul(
                             out=folded[:, jj, :],
-                            lhsT=log_std[k, c][:, P * j : P * (j + 1)],
+                            lhsT=log_std[k][:, c, P * j : P * (j + 1)],
                             rhs=ident_f32[:],
                             is_transpose=True,
                             start=(c == 0),
@@ -280,12 +285,12 @@ def tile_deepgmm_pa_kernel(
         handed = keep.tile([P, CLUSTERS], F32)
 
         def side_ratio(k, mean):
-            ratio = side_pool.tile([P, ROWS], F32)
+            diff = side_pool.tile([P, ROWS], F32, name="side")
             nc.gpsimd.tensor_scalar(
-                out=ratio[:], in0=mu_t[:, GPSIMD_CHUNK, :], scalar1=1.0, scalar2=mean, op0=ALU.mult, op1=ALU.add
+                out=diff[:], in0=mu_t[:, GPSIMD_CHUNK, :], scalar1=1.0, scalar2=mean, op0=ALU.mult, op1=ALU.add
             )
-            nc.gpsimd.tensor_tensor(out=ratio[:], in0=ratio[:], in1=inv_std[k, GPSIMD_CHUNK][:], op=ALU.mult)
-            ratios[k, GPSIMD_CHUNK] = ratio
+            ratio = ratios[k][:, GPSIMD_CHUNK, :]
+            nc.gpsimd.tensor_tensor(out=ratio, in0=diff[:], in1=ratio, op=ALU.mult)
 
         def hand_on(k, batch):
             if k + 1 in batch:
@@ -295,23 +300,22 @@ def tile_deepgmm_pa_kernel(
         def form_ratios(k):
             for c in range(DIM_CHUNKS):
                 if c != GPSIMD_CHUNK:
-                    ratio = ratio_pool.tile([P, ROWS], F32)
+                    ratio = ratios[k][:, c, :]
                     nc.vector.scalar_tensor_tensor(
-                        out=ratio[:],
+                        out=ratio,
                         in0=mu_t[:, c, :],
                         scalar=small[:, c, k : k + 1],
-                        in1=inv_std[k, c][:],
+                        in1=ratio,
                         op0=ALU.subtract,
                         op1=ALU.mult,
                     )
-                    ratios[k, c] = ratio
 
         def sum_squares(k):
             share = scalar_share[k - CLUSTERS] if k >= CLUSTERS - len(scalar_share) else 0
             for j in range(ROW_TILES):
                 turned = turn_pool.tile([P, DIM], F32, name="turned")
                 for c in range(DIM_CHUNKS):
-                    nc.tensor.transpose(turned[:, P * c : P * (c + 1)], ratios[k, c][:, P * j : P * (j + 1)], ident_f32[:])
+                    nc.tensor.transpose(turned[:, P * c : P * (c + 1)], ratios[k][:, c, P * j : P * (j + 1)], ident_f32[:])
                 if j >= ROW_TILES - share:
                     nc.scalar.activation(out=waste[:], in_=turned[:], func=ACT.Square, accum_out=squares[:, k, j : j + 1])
                 else:
@@ -323,6 +327,7 @@ def tile_deepgmm_pa_kernel(
             batches.append(list(range(first, first + size)))
             first += size
         batches.append([])
+        starts = [batch[0] for batch in batches if batch]
 
         def cluster(k, batch):
             form_ratios(k)

@@ -25,7 +25,9 @@ PASSES = K_IN // K_PASS
 BANK = 512
 ROW_HALVES = ROWS // BANK
 BATCHES = (5, 4, 4, 3)
+GRAMS = 12
 WIDE = 4
+EARLIER = 13
 GPSIMD_CHUNKS = (0,)
 EXP_CAP = 1.0e13
 SIG_FLOOR = 0.001
@@ -70,13 +72,15 @@ def tile_deepgmm_pa_kernel(
         neg_mean = keep.tile([P, DIM_CHUNKS, CLUSTERS], F32)
         logits = keep.tile([P, CLUSTERS], BF16)
 
-        held = ctx.enter_context(tc.tile_pool(name="held", bufs=1))
+        log_pool = ctx.enter_context(tc.tile_pool(name="log_std", bufs=5))
+        side_pool = ctx.enter_context(tc.tile_pool(name="side", bufs=2))
+        stage_pool = ctx.enter_context(tc.tile_pool(name="stage", bufs=3))
         with tc.tile_pool(name="enc", bufs=1) as enc, tc.psum_pool(name="enc_turn", bufs=4) as enc_turn, tc.psum_pool(
             name="enc_acc", bufs=4
         ) as enc_acc:
             y_sb = enc.tile([P, ROW_TILES, K_IN], BF16)
-            w_words = held.tile([P, 2, PASSES, DIM], U32, align_bytes=64)
-            w_scales = held.tile([P, 2, PASSES, DIM], U8, align_bytes=64)
+            w_words = enc.tile([P, 2, PASSES, DIM], U32, align_bytes=64)
+            w_scales = enc.tile([P, 2, PASSES, DIM], U8, align_bytes=64)
             small_rows = enc.tile([P, DIM], BF16)
 
             nc.vector.memset(small_rows[:], 0.0)
@@ -105,17 +109,17 @@ def tile_deepgmm_pa_kernel(
             nc.sync.dma_start(out=small_rows[32:33, :], in_=be_mu.unsqueeze(0))
             nc.sync.dma_start(out=small_rows[33:34, :], in_=be_sig.unsqueeze(0))
             load_rows(2)
-            load_weight(0, We_sig_words, We_sig_scales)
             load_rows(4)
             load_rows(6)
+            load_weight(0, We_sig_words, We_sig_scales)
             load_weight(1, We_mu_words, We_mu_scales)
             nc.sync.dma_start(out=logits[:], in_=phi_logits.partition_broadcast(P))
 
             y_words = y_sb[:].bitcast(F32)
             grouped = enc.tile([P, PASSES, ROWS, 4], BF16, align_bytes=64)
             grouped_words = grouped[:].rearrange("p g n t -> p g (n t)").bitcast(F32)
-            y_codes = held.tile([P, PASSES, ROWS], U32, align_bytes=64)
-            y_scales = held.tile([P, PASSES, ROWS], U8, align_bytes=64)
+            y_codes = enc.tile([P, PASSES, ROWS], U32, align_bytes=64)
+            y_scales = enc.tile([P, PASSES, ROWS], U8, align_bytes=64)
             def turn_pair(j, scalar_helps):
                 if True:
                     for g in range(PASSES):
@@ -152,8 +156,8 @@ def tile_deepgmm_pa_kernel(
                 nc.vector.tensor_scalar_add(out=std_bias[:], in0=small[:, :, 16:32], scalar1=SIG_FLOOR)
                 nc.vector.tensor_scalar_mul(out=neg_mean[:], in0=small[:, :, 0:16], scalar1=-1.0)
 
-            def product(w, c, h):
-                acc = enc_acc.tile([P, BANK], F32)
+            def product(w, c, h, pool, name):
+                acc = pool.tile([P, BANK], F32, name=name)
                 dims = slice(P * c, P * (c + 1))
                 rows_h = slice(BANK * h, BANK * (h + 1))
                 for g in range(PASSES):
@@ -168,47 +172,56 @@ def tile_deepgmm_pa_kernel(
                     )
                 return acc
 
-            pre = enc.tile([P, DIM_CHUNKS, ROWS], F32)
+            sums = {}
             soft = enc.tile([P, DIM_CHUNKS, ROWS], F32)
 
             def sigma_bank(h, c):
                 rows_h = slice(BANK * h, BANK * (h + 1))
-                acc = product(0, c, h)
-                nc.scalar.activation(out=soft[:, c, rows_h], in_=acc[:], func=ACT.Exp, bias=small[:, c, 33:34])
-                nc.vector.tensor_scalar_add(out=pre[:, c, rows_h], in0=acc[:], scalar1=small[:, c, 33:34])
+                pool, name = ((enc_acc, "acc"), (enc_turn, "turned"))[h]
+                sums[c, h] = product(0, c, h, pool, name)
+                nc.scalar.activation(
+                    out=soft[:, c, rows_h], in_=sums[c, h][:], func=ACT.Exp, bias=small[:, c, 33:34]
+                )
                 if h == 1:
-                    nc.vector.tensor_scalar_min(out=soft[:, c, :], in0=soft[:, c, :], scalar1=EXP_CAP)
+                    nc.vector.tensor_scalar_min(out=soft[:, c, rows_h], in0=soft[:, c, rows_h], scalar1=EXP_CAP)
 
             turn_pair(0, True)
             turn_pair(2, True)
             quantize_half(0)
             turn_small()
-            turn_pair(4, False)
+            turn_pair(4, True)
+            turn_pair(6, True)
+            quantize_half(1)
             sigma_bank(0, 0)
             sigma_bank(0, 1)
-            turn_pair(6, False)
-            quantize_half(1)
             sigma_bank(0, 2)
             sigma_bank(0, 3)
+            nc.vector.tensor_scalar_min(out=soft[:, :, 0:BANK], in0=soft[:, :, 0:BANK], scalar1=EXP_CAP)
             for c in range(DIM_CHUNKS):
                 sigma_bank(1, c)
 
             def mean_bank(h, c):
                 rows_h = slice(BANK * h, BANK * (h + 1))
-                acc = product(1, c, h)
+                acc = product(1, c, h, enc_acc, "acc")
                 nc.vector.tensor_scalar_add(out=mu_t[:, c, rows_h], in0=acc[:], scalar1=small[:, c, 32:33])
 
             for c in range(DIM_CHUNKS):
                 nc.scalar.activation(out=soft[:, c, :], in_=soft[:, c, :], func=ACT.Ln, bias=1.0)
-                nc.vector.tensor_max(out=sp_t[:, c, :], in0=soft[:, c, :], in1=pre[:, c, :])
+                for h in range(ROW_HALVES):
+                    rows_h = slice(BANK * h, BANK * (h + 1))
+                    nc.vector.scalar_tensor_tensor(
+                        out=sp_t[:, c, rows_h],
+                        in0=sums[c, h][:],
+                        scalar=small[:, c, 33:34],
+                        in1=soft[:, c, rows_h],
+                        op0=ALU.add,
+                        op1=ALU.max,
+                    )
             for h in range(ROW_HALVES):
                 for c in range(DIM_CHUNKS):
                     mean_bank(h, c)
 
-        log_pool = ctx.enter_context(tc.tile_pool(name="log_std", bufs=5))
-        ratio_pool = ctx.enter_context(tc.tile_pool(name="ratio", bufs=4))
-        side_pool = ctx.enter_context(tc.tile_pool(name="side", bufs=2))
-        stage_pool = ctx.enter_context(tc.tile_pool(name="stage", bufs=2))
+        ratio_pool = ctx.enter_context(tc.tile_pool(name="ratio", bufs=5))
         turn_pool = ctx.enter_context(tc.psum_pool(name="turn", bufs=6))
         fold_pool = ctx.enter_context(tc.psum_pool(name="fold", bufs=2))
 
@@ -237,6 +250,7 @@ def tile_deepgmm_pa_kernel(
         nc.vector.memset(moments[:], 0.0)
         squares = keep.tile([P, CLUSTERS, ROW_TILES], F32)
         nc.vector.memset(squares[:], 0.0)
+        waste_v = keep.tile([P, P], F32)
         waste = keep.tile([P, DIM], F32)
 
         log_std = {}
@@ -313,6 +327,23 @@ def tile_deepgmm_pa_kernel(
         def sum_squares(k):
             share = scalar_share[k - CLUSTERS] if k >= CLUSTERS - len(scalar_share) else 0
             for j in range(ROW_TILES):
+                if k < GRAMS and j == ROW_TILES - 1:
+                    gram = turn_pool.tile([P, P], F32, name="turned")
+                    for c in range(DIM_CHUNKS):
+                        ratio = ratios[k][:, c, P * j : P * (j + 1)]
+                        nc.tensor.matmul(
+                            out=gram[:], lhsT=ratio, rhs=ratio, start=(c == 0), stop=(c == DIM_CHUNKS - 1)
+                        )
+                    nc.vector.scalar_tensor_tensor(
+                        out=waste_v[:],
+                        in0=gram[:],
+                        scalar=1.0,
+                        in1=ident_f32[:],
+                        op0=ALU.mult,
+                        op1=ALU.mult,
+                        accum_out=squares[:, k, j : j + 1],
+                    )
+                    continue
                 turned = turn_pool.tile([P, DIM], F32, name="turned")
                 for c in range(DIM_CHUNKS):
                     nc.tensor.transpose(turned[:, P * c : P * (c + 1)], ratios[k][:, c, P * j : P * (j + 1)], ident_f32[:])
@@ -359,38 +390,46 @@ def tile_deepgmm_pa_kernel(
                 inverses_of([k + 1])
             cluster(k, batch)
 
-        cells = CLUSTERS * ROW_TILES
-        halves = moments[:].rearrange("p k j (e s) -> p (k j e) s", s=3)
-        mean_sq = keep.tile([P, 2 * cells], F32)
-        nc.vector.tensor_mul(out=mean_sq[:], in0=halves[:, :, 1], in1=halves[:, :, 1])
-        half_sums = keep.tile([P, cells, 2], F32)
-        nc.vector.scalar_tensor_tensor(
-            out=half_sums[:].rearrange("p x e -> p (x e)"),
-            in0=mean_sq[:],
-            scalar=float(DIM // 2),
-            in1=halves[:, :, 2],
-            op0=ALU.mult,
-            op1=ALU.add,
+        def half_views(first, last):
+            halves = moments[:, first:last, :, :].rearrange("p k j (e s) -> p (k j e) s", s=3)
+            sums = keep.tile([P, 2 * (last - first) * ROW_TILES], F32, name="half_sums%d" % first)
+            energy = keep.tile([P, last - first, ROW_TILES], F32, name="energy%d" % first)
+            return halves[:, :, 1], halves[:, :, 2], sums[:], energy
+
+        mean, spread, sums, early = half_views(0, EARLIER)
+        flat = early[:].rearrange("p k j -> p (k j)")
+        pairs = sums.rearrange("p (x e) -> p x e", e=2)
+        nc.gpsimd.tensor_tensor(out=sums, in0=mean, in1=mean, op=ALU.mult)
+        nc.gpsimd.tensor_scalar(
+            out=sums, in0=sums, scalar1=float(DIM // 2), scalar2=0.0, op0=ALU.mult, op1=ALU.add
         )
-        quad_form = keep.tile([P, cells], F32)
-        nc.vector.tensor_reduce(out=quad_form[:], in_=half_sums[:], axis=AXIS_X, op=ALU.add)
-        nc.vector.tensor_add(out=quad_form[:], in0=quad_form[:], in1=squares[:].rearrange("p k j -> p (k j)"))
-        by_cluster = keep.tile([P, CLUSTERS, ROW_TILES], F32)
+        nc.gpsimd.tensor_tensor(out=sums, in0=sums, in1=spread, op=ALU.add)
+        nc.gpsimd.tensor_tensor(out=flat, in0=pairs[:, :, 0], in1=pairs[:, :, 1], op=ALU.add)
+        nc.gpsimd.tensor_tensor(out=early[:], in0=early[:], in1=squares[:, 0:EARLIER, :], op=ALU.add)
+        nc.gpsimd.tensor_scalar(out=flat, in0=flat, scalar1=-0.5, scalar2=0.0, op0=ALU.mult, op1=ALU.add)
+        nc.gpsimd.tensor_tensor(out=early[:], in0=early[:], in1=log_det[:, 0:EARLIER, :], op=ALU.subtract)
+
+        mean, spread, sums, late = half_views(EARLIER, CLUSTERS)
+        flat = late[:].rearrange("p k j -> p (k j)")
+        pairs = sums.rearrange("p (x e) -> p x e", e=2)
+        nc.vector.tensor_tensor(out=sums, in0=mean, in1=mean, op=ALU.mult)
         nc.vector.scalar_tensor_tensor(
-            out=by_cluster[:].rearrange("p k j -> p (k j)"),
-            in0=quad_form[:],
-            scalar=-0.5,
-            in1=log_det[:].rearrange("p k j -> p (k j)"),
-            op0=ALU.mult,
-            op1=ALU.subtract,
+            out=sums, in0=sums, scalar=float(DIM // 2), in1=spread, op0=ALU.mult, op1=ALU.add
         )
+        nc.vector.tensor_tensor(out=flat, in0=pairs[:, :, 0], in1=pairs[:, :, 1], op=ALU.add)
+        nc.vector.tensor_tensor(out=late[:], in0=late[:], in1=squares[:, EARLIER:CLUSTERS, :], op=ALU.add)
+        nc.vector.scalar_tensor_tensor(
+            out=late[:], in0=late[:], scalar=-0.5, in1=log_det[:, EARLIER:CLUSTERS, :], op0=ALU.mult, op1=ALU.subtract
+        )
+
         z = keep.tile([P, ROW_TILES, CLUSTERS], F32)
-        nc.vector.tensor_tensor(
-            out=z[:],
-            in0=by_cluster[:].rearrange("p k j -> p j k"),
-            in1=logits[:].unsqueeze(1).to_broadcast([P, ROW_TILES, CLUSTERS]),
-            op=ALU.add,
-        )
+        for first, last, energy in ((0, EARLIER, early), (EARLIER, CLUSTERS, late)):
+            nc.vector.tensor_tensor(
+                out=z[:, :, first:last],
+                in0=energy[:].rearrange("p k j -> p j k"),
+                in1=logits[:, first:last].unsqueeze(1).to_broadcast([P, ROW_TILES, last - first]),
+                op=ALU.add,
+            )
         z_max = keep.tile([P, ROW_TILES], F32)
         nc.vector.tensor_reduce(out=z_max[:], in_=z[:], axis=AXIS_X, op=ALU.max)
         nc.vector.tensor_tensor(

@@ -26,7 +26,7 @@ BANK = 512
 ROW_HALVES = ROWS // BANK
 BATCHES = (5, 4, 4, 3)
 GRAMS = 12
-WIDE = 4
+PAIRED = 2
 EARLIER = 13
 GPSIMD_CHUNKS = (0,)
 EXP_CAP = 1.0e13
@@ -257,19 +257,40 @@ def tile_deepgmm_pa_kernel(
         ratios = {}
         scalar_share = (4, 4, 4)
 
+        def terms_of(k):
+            return DIM_CHUNKS - 1 if k < PAIRED else DIM_CHUNKS
+
         def logs_of(batch):
             for k in batch:
                 log_std[k] = log_pool.tile([P, DIM_CHUNKS, ROWS], F32, name="logs")
-                for c in range(DIM_CHUNKS):
+            for k in batch:
+                for c in range(DIM_CHUNKS - 2 if k < PAIRED else DIM_CHUNKS):
                     nc.scalar.activation(
                         out=log_std[k][:, c, :], in_=sp_t[:, c, :], func=ACT.Ln, bias=std_bias[:, c, k : k + 1]
                     )
+            for k in batch:
+                if k < PAIRED:
+                    factor = side_pool.tile([P, ROWS], F32, name="side")
+                    for c, std in ((DIM_CHUNKS - 2, factor[:]), (DIM_CHUNKS - 1, log_std[k][:, DIM_CHUNKS - 1, :])):
+                        nc.gpsimd.tensor_scalar(
+                            out=std,
+                            in0=sp_t[:, c, :],
+                            scalar1=1.0,
+                            scalar2=std_bias[:, c, k : k + 1],
+                            op0=ALU.mult,
+                            op1=ALU.add,
+                        )
+                    product = log_std[k][:, DIM_CHUNKS - 2, :]
+                    nc.gpsimd.tensor_tensor(
+                        out=product, in0=factor[:], in1=log_std[k][:, DIM_CHUNKS - 1, :], op=ALU.mult
+                    )
+                    nc.scalar.activation(out=product, in_=product, func=ACT.Ln)
 
         def inverses_of(batch):
             for k in batch:
                 ratios[k] = ratio_pool.tile([P, DIM_CHUNKS, ROWS], F32, name="ratio")
-                step = 1 if k in starts else WIDE
-                for c in range(0, DIM_CHUNKS, step):
+                step = 1 if k in starts else terms_of(k)
+                for c in range(0, terms_of(k), step):
                     nc.scalar.activation(
                         out=ratios[k][:, c : c + step, :],
                         in_=log_std[k][:, c : c + step, :],
@@ -282,14 +303,14 @@ def tile_deepgmm_pa_kernel(
                 folded = fold_pool.tile([P, 4, P], F32)
                 for jj in range(4):
                     j = 4 * half + jj
-                    for c in range(DIM_CHUNKS):
+                    for c in range(terms_of(k)):
                         nc.tensor.matmul(
                             out=folded[:, jj, :],
                             lhsT=log_std[k][:, c, P * j : P * (j + 1)],
                             rhs=ident_f32[:],
                             is_transpose=True,
                             start=(c == 0),
-                            stop=(c == DIM_CHUNKS - 1),
+                            stop=(c == terms_of(k) - 1),
                         )
                 nc.vector.tensor_reduce(
                     out=log_det[:, k, 4 * half : 4 * half + 4], in_=folded[:], axis=AXIS_X, op=ALU.add
@@ -311,18 +332,37 @@ def tile_deepgmm_pa_kernel(
                 nc.vector.tensor_copy(out=handed[:, k + 1 : k + 2], in_=neg_mean[:, GPSIMD_CHUNK, k + 1 : k + 2])
                 side_ratio(k + 1, handed[:, k + 1 : k + 2])
 
+        def scaled_difference(k, c, source):
+            nc.vector.scalar_tensor_tensor(
+                out=ratios[k][:, c, :],
+                in0=mu_t[:, c, :],
+                scalar=small[:, c, k : k + 1],
+                in1=ratios[k][:, source, :],
+                op0=ALU.subtract,
+                op1=ALU.mult,
+            )
+
         def form_ratios(k):
-            for c in range(DIM_CHUNKS):
-                if c != GPSIMD_CHUNK:
-                    ratio = ratios[k][:, c, :]
-                    nc.vector.scalar_tensor_tensor(
-                        out=ratio,
-                        in0=mu_t[:, c, :],
-                        scalar=small[:, c, k : k + 1],
-                        in1=ratio,
-                        op0=ALU.subtract,
-                        op1=ALU.mult,
-                    )
+            if k < PAIRED:
+                a, b = DIM_CHUNKS - 2, DIM_CHUNKS - 1
+                for c in range(1, a):
+                    scaled_difference(k, c, c)
+                scaled_difference(k, b, a)
+                scaled_difference(k, a, a)
+                nc.vector.scalar_tensor_tensor(
+                    out=ratios[k][:, b, :],
+                    in0=sp_t[:, a, :],
+                    scalar=std_bias[:, a, k : k + 1],
+                    in1=ratios[k][:, b, :],
+                    op0=ALU.add,
+                    op1=ALU.mult,
+                )
+                nc.vector.tensor_tensor(
+                    out=ratios[k][:, a, :], in0=log_std[k][:, b, :], in1=ratios[k][:, a, :], op=ALU.mult
+                )
+            else:
+                for c in range(1, DIM_CHUNKS):
+                    scaled_difference(k, c, c)
 
         def sum_squares(k):
             share = scalar_share[k - CLUSTERS] if k >= CLUSTERS - len(scalar_share) else 0
@@ -357,20 +397,19 @@ def tile_deepgmm_pa_kernel(
         for size in BATCHES:
             batches.append(list(range(first, first + size)))
             first += size
-        batches.append([])
-        starts = [batch[0] for batch in batches if batch]
+        starts = [batch[0] for batch in batches]
 
         def cluster(k, batch):
             form_ratios(k)
             hand_on(k, batch)
-            if k >= BATCHES[0]:
+            if k >= BATCHES[0] or k < PAIRED:
                 sum_logs(k)
             sum_squares(k)
 
-        for batch in batches[0 : len(BATCHES) - 1]:
+        for batch in batches:
             logs_of(batch)
             if batch is batches[0]:
-                for k in batch:
+                for k in batch[PAIRED:]:
                     for twice in range(2):
                         if stores:
                             store_pair(*stores.pop(0))
@@ -381,14 +420,6 @@ def tile_deepgmm_pa_kernel(
             side_ratio(batch[0], neg_mean[:, GPSIMD_CHUNK, batch[0] : batch[0] + 1])
             for k in batch:
                 cluster(k, batch)
-        batch = batches[len(BATCHES) - 1]
-        logs_of(batch)
-        inverses_of(batch[0 : 1])
-        side_ratio(batch[0], neg_mean[:, GPSIMD_CHUNK, batch[0] : batch[0] + 1])
-        for k in batch:
-            if k + 1 in batch:
-                inverses_of([k + 1])
-            cluster(k, batch)
 
         def half_views(first, last):
             halves = moments[:, first:last, :, :].rearrange("p k j (e s) -> p (k j e) s", s=3)

@@ -27,6 +27,7 @@ ROW_HALVES = ROWS // BANK
 BATCHES = (5, 4, 4, 3)
 GRAMS = 12
 PAIRED = 2
+EXTRA = 128
 EARLIER = 13
 GPSIMD_CHUNKS = (0,)
 EXP_CAP = 1.0e13
@@ -255,7 +256,7 @@ def tile_deepgmm_pa_kernel(
 
         log_std = {}
         ratios = {}
-        scalar_share = (4, 4, 4)
+        scalar_share = (3, 4, 4)
 
         def terms_of(k):
             return DIM_CHUNKS - 1 if k < PAIRED else DIM_CHUNKS
@@ -326,18 +327,29 @@ def tile_deepgmm_pa_kernel(
             )
             ratio = ratios[k][:, GPSIMD_CHUNK, :]
             nc.gpsimd.tensor_tensor(out=ratio, in0=diff[:], in1=ratio, op=ALU.mult)
+            rows = slice(ROWS - EXTRA, ROWS)
+            nc.gpsimd.tensor_scalar(
+                out=diff[:, 0:EXTRA],
+                in0=mu_t[:, 1, rows],
+                scalar1=1.0,
+                scalar2=neg_mean[:, 1, k : k + 1],
+                op0=ALU.mult,
+                op1=ALU.add,
+            )
+            part = ratios[k][:, 1, rows]
+            nc.gpsimd.tensor_tensor(out=part, in0=diff[:, 0:EXTRA], in1=part, op=ALU.mult)
 
         def hand_on(k, batch):
             if k + 1 in batch:
                 nc.vector.tensor_copy(out=handed[:, k + 1 : k + 2], in_=neg_mean[:, GPSIMD_CHUNK, k + 1 : k + 2])
                 side_ratio(k + 1, handed[:, k + 1 : k + 2])
 
-        def scaled_difference(k, c, source):
+        def scaled_difference(k, c, source, rows=slice(0, ROWS)):
             nc.vector.scalar_tensor_tensor(
-                out=ratios[k][:, c, :],
-                in0=mu_t[:, c, :],
+                out=ratios[k][:, c, rows],
+                in0=mu_t[:, c, rows],
                 scalar=small[:, c, k : k + 1],
-                in1=ratios[k][:, source, :],
+                in1=ratios[k][:, source, rows],
                 op0=ALU.subtract,
                 op1=ALU.mult,
             )
@@ -345,8 +357,7 @@ def tile_deepgmm_pa_kernel(
         def form_ratios(k):
             if k < PAIRED:
                 a, b = DIM_CHUNKS - 2, DIM_CHUNKS - 1
-                for c in range(1, a):
-                    scaled_difference(k, c, c)
+                scaled_difference(k, 1, 1, slice(0, ROWS - EXTRA))
                 scaled_difference(k, b, a)
                 scaled_difference(k, a, a)
                 nc.vector.scalar_tensor_tensor(
@@ -361,7 +372,8 @@ def tile_deepgmm_pa_kernel(
                     out=ratios[k][:, a, :], in0=log_std[k][:, b, :], in1=ratios[k][:, a, :], op=ALU.mult
                 )
             else:
-                for c in range(1, DIM_CHUNKS):
+                scaled_difference(k, 1, 1, slice(0, ROWS - EXTRA))
+                for c in range(2, DIM_CHUNKS):
                     scaled_difference(k, c, c)
 
         def sum_squares(k):

from contextlib import ExitStack

import concourse.mybir as mybir
from concourse.masks import make_identity

F32 = mybir.dt.float32
BF16 = mybir.dt.bfloat16
I32 = mybir.dt.int32
U32 = mybir.dt.uint32
U8 = mybir.dt.uint8
FP8X4 = mybir.dt.float8_e4m3fn_x4
ACT = mybir.ActivationFunctionType
ALU = mybir.AluOpType
AXIS_X = mybir.AxisListType.X

P = 128
ROWS = 1024
K_IN = 1024
DIM = 512
CLUSTERS = 16
ROW_TILES = ROWS // P
DIM_CHUNKS = DIM // P
K_PASS = 4 * P
PASSES = K_IN // K_PASS
BANK = 512
ROW_HALVES = ROWS // BANK
BATCHES = (5, 4, 4, 3)
GRAMS = 12
PAIRED = 2
EXTRA = 128
EARLIER = 13
GPSIMD_CHUNKS = (0,)
EXP_CAP = 1.0e13
SIG_FLOOR = 0.001

FLOPS = 2 * 2 * ROWS * K_IN * DIM


def tile_deepgmm_pa_kernel(
    tc,
    Y,
    We_mu_words,
    We_mu_scales,
    be_mu,
    We_sig_words,
    We_sig_scales,
    be_sig,
    phi_mus,
    phi_sigs,
    phi_logits,
    out_0,
    out_1,
    out_2,
):
    nc = tc.nc
    with ExitStack() as ctx:
        ctx.enter_context(tc.manual_schedule())
        keep = ctx.enter_context(tc.tile_pool(name="keep", bufs=1))

        spark = keep.tile([P, 1], F32)
        nc.vector.memset(spark[:], 0.0)
        nc.scalar.activation(out=spark[:], in_=spark[:], func=ACT.Exp)

        ident_f32 = keep.tile([P, P], F32)
        make_identity(nc, ident_f32[:])
        ident_bf16 = keep.tile([P, P], BF16)
        make_identity(nc, ident_bf16[:])

        mu_t = keep.tile([P, DIM_CHUNKS, ROWS], F32)
        sp_t = keep.tile([P, DIM_CHUNKS, ROWS], F32)
        small = keep.tile([P, DIM_CHUNKS, 34], F32)
        std_bias = keep.tile([P, DIM_CHUNKS, CLUSTERS], F32)
        neg_mean = keep.tile([P, DIM_CHUNKS, CLUSTERS], F32)
        logits = keep.tile([P, CLUSTERS], BF16)

        log_pool = ctx.enter_context(tc.tile_pool(name="log_std", bufs=5))
        side_pool = ctx.enter_context(tc.tile_pool(name="side", bufs=2))
        stage_pool = ctx.enter_context(tc.tile_pool(name="stage", bufs=3))
        with tc.tile_pool(name="enc", bufs=1) as enc, tc.psum_pool(name="enc_turn", bufs=4) as enc_turn, tc.psum_pool(
            name="enc_acc", bufs=4
        ) as enc_acc:
            y_sb = enc.tile([P, ROW_TILES, K_IN], BF16)
            w_words = enc.tile([P, 2, PASSES, DIM], U32, align_bytes=64)
            w_scales = enc.tile([P, 2, PASSES, DIM], U8, align_bytes=64)
            small_rows = enc.tile([P, DIM], BF16)

            nc.vector.memset(small_rows[:], 0.0)
            nc.vector.memset(w_scales[:].rearrange("p w g n -> p (w g n)").bitcast(I32), 0)

            y_rows = Y.rearrange("(p j) k -> p j k", j=ROW_TILES)

            def load_rows(j):
                nc.sync.dma_start(out=y_sb[:, j : j + 2, :], in_=y_rows[:, j : j + 2, :])

            def load_weight(w, words, scales):
                for g in range(PASSES):
                    nc.sync.dma_start(
                        out=w_words[:, w, g, :].bitcast(I32),
                        in_=words[g].rearrange("p n t -> p (n t)").bitcast(I32),
                    )
                for quad in range(4):
                    nc.sync.dma_start(
                        out=w_scales[32 * quad : 32 * quad + 4, w, :, :].bitcast(I32),
                        in_=scales[:, 4 * quad : 4 * quad + 4, :].rearrange("g r n -> r g n").bitcast(I32),
                    )

            load_rows(0)
            nc.sync.dma_start(out=small_rows[0:16, :], in_=phi_mus)
            nc.sync.dma_start(out=small_rows[16:32, :], in_=phi_sigs)
            nc.sync.dma_start(out=small_rows[32:33, :], in_=be_mu.unsqueeze(0))
            nc.sync.dma_start(out=small_rows[33:34, :], in_=be_sig.unsqueeze(0))
            load_rows(2)
            load_rows(4)
            load_rows(6)
            load_weight(0, We_sig_words, We_sig_scales)
            load_weight(1, We_mu_words, We_mu_scales)
            nc.sync.dma_start(out=logits[:], in_=phi_logits.partition_broadcast(P))

            y_words = y_sb[:].bitcast(F32)
            grouped = enc.tile([P, PASSES, ROWS, 4], BF16, align_bytes=64)
            grouped_words = grouped[:].rearrange("p g n t -> p g (n t)").bitcast(F32)
            y_codes = enc.tile([P, PASSES, ROWS], U32, align_bytes=64)
            y_scales = enc.tile([P, PASSES, ROWS], U8, align_bytes=64)
            def turn_pair(j, scalar_helps):
                if True:
                    for g in range(PASSES):
                        turned = enc_turn.tile([P, 2, 2, P], F32, name="turned")
                        for jj in range(2):
                            for u in range(2):
                                nc.tensor.transpose(
                                    turned[:, jj, u, :],
                                    y_words[:, j + jj, 256 * g + u : 256 * (g + 1) : 2],
                                    ident_f32[:],
                                )
                        pairs = grouped_words[:, g, 2 * P * j : 2 * P * (j + 2)].rearrange(
                            "p (jj n u) -> p jj n u", jj=2, u=2
                        )
                        if g == 0 or not scalar_helps:
                            nc.vector.tensor_copy(out=pairs, in_=turned[:].rearrange("p jj u n -> p jj n u"))
                        else:
                            nc.scalar.copy(out=pairs, in_=turned[:].rearrange("p jj u n -> p jj n u"))

            def quantize_half(h):
                for g in range(PASSES):
                    rows_h = slice(BANK * h, BANK * (h + 1))
                    nc.vector.quantize_mx(
                        out=y_codes[:, g, rows_h].bitcast(FP8X4),
                        scales=y_scales[:, g, rows_h],
                        in_=grouped[:, g, rows_h, :].rearrange("p n t -> p (n t)"),
                    )

            def turn_small():
                small_t = enc_turn.tile([P, DIM_CHUNKS, P], BF16, name="turned")
                for c in range(DIM_CHUNKS):
                    nc.tensor.transpose(small_t[:, c, :], small_rows[:, P * c : P * (c + 1)], ident_bf16[:])
                nc.vector.tensor_copy(out=small[:], in_=small_t[:, :, 0:34])
                nc.vector.tensor_scalar_add(out=std_bias[:], in0=small[:, :, 16:32], scalar1=SIG_FLOOR)
                nc.vector.tensor_scalar_mul(out=neg_mean[:], in0=small[:, :, 0:16], scalar1=-1.0)

            def product(w, c, h, pool, name):
                acc = pool.tile([P, BANK], F32, name=name)
                dims = slice(P * c, P * (c + 1))
                rows_h = slice(BANK * h, BANK * (h + 1))
                for g in range(PASSES):
                    nc.tensor.matmul_mx(
                        out=acc[:],
                        lhsT=w_words[:, w, g, dims].bitcast(FP8X4),
                        lhsT_scale=w_scales[:, w, g, dims],
                        rhs=y_codes[:, g, rows_h].bitcast(FP8X4),
                        rhs_scale=y_scales[:, g, rows_h],
                        start=(g == 0),
                        stop=(g == PASSES - 1),
                    )
                return acc

            sums = {}
            soft = enc.tile([P, DIM_CHUNKS, ROWS], F32)

            def sigma_bank(h, c):
                rows_h = slice(BANK * h, BANK * (h + 1))
                pool, name = ((enc_acc, "acc"), (enc_turn, "turned"))[h]
                sums[c, h] = product(0, c, h, pool, name)
                nc.scalar.activation(
                    out=soft[:, c, rows_h], in_=sums[c, h][:], func=ACT.Exp, bias=small[:, c, 33:34]
                )
                if h == 1:
                    nc.vector.tensor_scalar_min(out=soft[:, c, rows_h], in0=soft[:, c, rows_h], scalar1=EXP_CAP)

            turn_pair(0, True)
            turn_pair(2, True)
            quantize_half(0)
            turn_small()
            turn_pair(4, True)
            turn_pair(6, True)
            quantize_half(1)
            sigma_bank(0, 0)
            sigma_bank(0, 1)
            sigma_bank(0, 2)
            sigma_bank(0, 3)
            nc.vector.tensor_scalar_min(out=soft[:, :, 0:BANK], in0=soft[:, :, 0:BANK], scalar1=EXP_CAP)
            for c in range(DIM_CHUNKS):
                sigma_bank(1, c)

            def mean_bank(h, c):
                rows_h = slice(BANK * h, BANK * (h + 1))
                acc = product(1, c, h, enc_acc, "acc")
                nc.vector.tensor_scalar_add(out=mu_t[:, c, rows_h], in0=acc[:], scalar1=small[:, c, 32:33])

            for c in range(DIM_CHUNKS):
                nc.scalar.activation(out=soft[:, c, :], in_=soft[:, c, :], func=ACT.Ln, bias=1.0)
                for h in range(ROW_HALVES):
                    rows_h = slice(BANK * h, BANK * (h + 1))
                    nc.vector.scalar_tensor_tensor(
                        out=sp_t[:, c, rows_h],
                        in0=sums[c, h][:],
                        scalar=small[:, c, 33:34],
                        in1=soft[:, c, rows_h],
                        op0=ALU.add,
                        op1=ALU.max,
                    )
            for h in range(ROW_HALVES):
                for c in range(DIM_CHUNKS):
                    mean_bank(h, c)

        ratio_pool = ctx.enter_context(tc.tile_pool(name="ratio", bufs=5))
        turn_pool = ctx.enter_context(tc.psum_pool(name="turn", bufs=6))
        fold_pool = ctx.enter_context(tc.psum_pool(name="fold", bufs=2))

        def store_pair(source, floor, target, first):
            stage = stage_pool.tile([P, 2, DIM], F32)
            for jj in range(2):
                j = first + jj
                turned = turn_pool.tile([P, DIM], F32, name="turned")
                for c in range(DIM_CHUNKS):
                    nc.tensor.transpose(
                        turned[:, P * c : P * (c + 1)], source[:, c, P * j : P * (j + 1)], ident_f32[:]
                    )
                nc.vector.tensor_scalar_add(out=stage[:, jj, :], in0=turned[:], scalar1=floor)
            nc.sync.dma_start(
                out=target.rearrange("(p j) d -> p j d", j=ROW_TILES)[:, first : first + 2, :], in_=stage[:]
            )

        stores = [
            (source, floor, target, first)
            for source, floor, target in ((mu_t, 0.0, out_0), (sp_t, SIG_FLOOR, out_1))
            for first in range(0, ROW_TILES, 2)
        ]

        log_det = keep.tile([P, CLUSTERS, ROW_TILES], F32)
        moments = keep.tile([P, CLUSTERS, ROW_TILES, 6], F32)
        nc.vector.memset(moments[:], 0.0)
        squares = keep.tile([P, CLUSTERS, ROW_TILES], F32)
        nc.vector.memset(squares[:], 0.0)
        waste_v = keep.tile([P, P], F32)
        waste = keep.tile([P, DIM], F32)

        log_std = {}
        ratios = {}
        scalar_share = (3, 4, 4)

        def terms_of(k):
            return DIM_CHUNKS - 1 if k < PAIRED else DIM_CHUNKS

        def logs_of(batch):
            for k in batch:
                log_std[k] = log_pool.tile([P, DIM_CHUNKS, ROWS], F32, name="logs")
            for k in batch:
                for c in range(DIM_CHUNKS - 2 if k < PAIRED else DIM_CHUNKS):
                    nc.scalar.activation(
                        out=log_std[k][:, c, :], in_=sp_t[:, c, :], func=ACT.Ln, bias=std_bias[:, c, k : k + 1]
                    )
            for k in batch:
                if k < PAIRED:
                    factor = side_pool.tile([P, ROWS], F32, name="side")
                    for c, std in ((DIM_CHUNKS - 2, factor[:]), (DIM_CHUNKS - 1, log_std[k][:, DIM_CHUNKS - 1, :])):
                        nc.gpsimd.tensor_scalar(
                            out=std,
                            in0=sp_t[:, c, :],
                            scalar1=1.0,
                            scalar2=std_bias[:, c, k : k + 1],
                            op0=ALU.mult,
                            op1=ALU.add,
                        )
                    product = log_std[k][:, DIM_CHUNKS - 2, :]
                    nc.gpsimd.tensor_tensor(
                        out=product, in0=factor[:], in1=log_std[k][:, DIM_CHUNKS - 1, :], op=ALU.mult
                    )
                    nc.scalar.activation(out=product, in_=product, func=ACT.Ln)

        def inverses_of(batch):
            for k in batch:
                ratios[k] = ratio_pool.tile([P, DIM_CHUNKS, ROWS], F32, name="ratio")
                step = 1 if k in starts else terms_of(k)
                for c in range(0, terms_of(k), step):
                    nc.scalar.activation(
                        out=ratios[k][:, c : c + step, :],
                        in_=log_std[k][:, c : c + step, :],
                        func=ACT.Exp,
                        scale=-1.0,
                    )

        def sum_logs(k):
            for half in range(2):
                folded = fold_pool.tile([P, 4, P], F32)
                for jj in range(4):
                    j = 4 * half + jj
                    for c in range(terms_of(k)):
                        nc.tensor.matmul(
                            out=folded[:, jj, :],
                            lhsT=log_std[k][:, c, P * j : P * (j + 1)],
                            rhs=ident_f32[:],
                            is_transpose=True,
                            start=(c == 0),
                            stop=(c == terms_of(k) - 1),
                        )
                nc.vector.tensor_reduce(
                    out=log_det[:, k, 4 * half : 4 * half + 4], in_=folded[:], axis=AXIS_X, op=ALU.add
                )

        GPSIMD_CHUNK = 0
        handed = keep.tile([P, CLUSTERS], F32)

        def side_ratio(k, mean):
            diff = side_pool.tile([P, ROWS], F32, name="side")
            nc.gpsimd.tensor_scalar(
                out=diff[:], in0=mu_t[:, GPSIMD_CHUNK, :], scalar1=1.0, scalar2=mean, op0=ALU.mult, op1=ALU.add
            )
            ratio = ratios[k][:, GPSIMD_CHUNK, :]
            nc.gpsimd.tensor_tensor(out=ratio, in0=diff[:], in1=ratio, op=ALU.mult)
            rows = slice(ROWS - EXTRA, ROWS)
            nc.gpsimd.tensor_scalar(
                out=diff[:, 0:EXTRA],
                in0=mu_t[:, 1, rows],
                scalar1=1.0,
                scalar2=neg_mean[:, 1, k : k + 1],
                op0=ALU.mult,
                op1=ALU.add,
            )
            part = ratios[k][:, 1, rows]
            nc.gpsimd.tensor_tensor(out=part, in0=diff[:, 0:EXTRA], in1=part, op=ALU.mult)

        def hand_on(k, batch):
            if k + 1 in batch:
                nc.vector.tensor_copy(out=handed[:, k + 1 : k + 2], in_=neg_mean[:, GPSIMD_CHUNK, k + 1 : k + 2])
                side_ratio(k + 1, handed[:, k + 1 : k + 2])

        def scaled_difference(k, c, source, rows=slice(0, ROWS)):
            nc.vector.scalar_tensor_tensor(
                out=ratios[k][:, c, rows],
                in0=mu_t[:, c, rows],
                scalar=small[:, c, k : k + 1],
                in1=ratios[k][:, source, rows],
                op0=ALU.subtract,
                op1=ALU.mult,
            )

        def form_ratios(k):
            if k < PAIRED:
                a, b = DIM_CHUNKS - 2, DIM_CHUNKS - 1
                scaled_difference(k, 1, 1, slice(0, ROWS - EXTRA))
                scaled_difference(k, b, a)
                scaled_difference(k, a, a)
                nc.vector.scalar_tensor_tensor(
                    out=ratios[k][:, b, :],
                    in0=sp_t[:, a, :],
                    scalar=std_bias[:, a, k : k + 1],
                    in1=ratios[k][:, b, :],
                    op0=ALU.add,
                    op1=ALU.mult,
                )
                nc.vector.tensor_tensor(
                    out=ratios[k][:, a, :], in0=log_std[k][:, b, :], in1=ratios[k][:, a, :], op=ALU.mult
                )
            else:
                scaled_difference(k, 1, 1, slice(0, ROWS - EXTRA))
                for c in range(2, DIM_CHUNKS):
                    scaled_difference(k, c, c)

        def sum_squares(k):
            share = scalar_share[k - CLUSTERS] if k >= CLUSTERS - len(scalar_share) else 0
            for j in range(ROW_TILES):
                if k < GRAMS and j == ROW_TILES - 1:
                    gram = turn_pool.tile([P, P], F32, name="turned")
                    for c in range(DIM_CHUNKS):
                        ratio = ratios[k][:, c, P * j : P * (j + 1)]
                        nc.tensor.matmul(
                            out=gram[:], lhsT=ratio, rhs=ratio, start=(c == 0), stop=(c == DIM_CHUNKS - 1)
                        )
                    nc.vector.scalar_tensor_tensor(
                        out=waste_v[:],
                        in0=gram[:],
                        scalar=1.0,
                        in1=ident_f32[:],
                        op0=ALU.mult,
                        op1=ALU.mult,
                        accum_out=squares[:, k, j : j + 1],
                    )
                    continue
                turned = turn_pool.tile([P, DIM], F32, name="turned")
                for c in range(DIM_CHUNKS):
                    nc.tensor.transpose(turned[:, P * c : P * (c + 1)], ratios[k][:, c, P * j : P * (j + 1)], ident_f32[:])
                if j >= ROW_TILES - share:
                    nc.scalar.activation(out=waste[:], in_=turned[:], func=ACT.Square, accum_out=squares[:, k, j : j + 1])
                else:
                    nc.vector.bn_stats(out=moments[:, k, j, :], in_=turned[:])

        batches = []
        first = 0
        for size in BATCHES:
            batches.append(list(range(first, first + size)))
            first += size
        starts = [batch[0] for batch in batches]

        def cluster(k, batch):
            form_ratios(k)
            hand_on(k, batch)
            if k >= BATCHES[0] or k < PAIRED:
                sum_logs(k)
            sum_squares(k)

        for batch in batches:
            logs_of(batch)
            if batch is batches[0]:
                for k in batch[PAIRED:]:
                    for twice in range(2):
                        if stores:
                            store_pair(*stores.pop(0))
                    sum_logs(k)
                while stores:
                    store_pair(*stores.pop(0))
            inverses_of(batch)
            side_ratio(batch[0], neg_mean[:, GPSIMD_CHUNK, batch[0] : batch[0] + 1])
            for k in batch:
                cluster(k, batch)

        def half_views(first, last):
            halves = moments[:, first:last, :, :].rearrange("p k j (e s) -> p (k j e) s", s=3)
            sums = keep.tile([P, 2 * (last - first) * ROW_TILES], F32, name="half_sums%d" % first)
            energy = keep.tile([P, last - first, ROW_TILES], F32, name="energy%d" % first)
            return halves[:, :, 1], halves[:, :, 2], sums[:], energy

        mean, spread, sums, early = half_views(0, EARLIER)
        flat = early[:].rearrange("p k j -> p (k j)")
        pairs = sums.rearrange("p (x e) -> p x e", e=2)
        nc.gpsimd.tensor_tensor(out=sums, in0=mean, in1=mean, op=ALU.mult)
        nc.gpsimd.tensor_scalar(
            out=sums, in0=sums, scalar1=float(DIM // 2), scalar2=0.0, op0=ALU.mult, op1=ALU.add
        )
        nc.gpsimd.tensor_tensor(out=sums, in0=sums, in1=spread, op=ALU.add)
        nc.gpsimd.tensor_tensor(out=flat, in0=pairs[:, :, 0], in1=pairs[:, :, 1], op=ALU.add)
        nc.gpsimd.tensor_tensor(out=early[:], in0=early[:], in1=squares[:, 0:EARLIER, :], op=ALU.add)
        nc.gpsimd.tensor_scalar(out=flat, in0=flat, scalar1=-0.5, scalar2=0.0, op0=ALU.mult, op1=ALU.add)
        nc.gpsimd.tensor_tensor(out=early[:], in0=early[:], in1=log_det[:, 0:EARLIER, :], op=ALU.subtract)

        mean, spread, sums, late = half_views(EARLIER, CLUSTERS)
        flat = late[:].rearrange("p k j -> p (k j)")
        pairs = sums.rearrange("p (x e) -> p x e", e=2)
        nc.vector.tensor_tensor(out=sums, in0=mean, in1=mean, op=ALU.mult)
        nc.vector.scalar_tensor_tensor(
            out=sums, in0=sums, scalar=float(DIM // 2), in1=spread, op0=ALU.mult, op1=ALU.add
        )
        nc.vector.tensor_tensor(out=flat, in0=pairs[:, :, 0], in1=pairs[:, :, 1], op=ALU.add)
        nc.vector.tensor_tensor(out=late[:], in0=late[:], in1=squares[:, EARLIER:CLUSTERS, :], op=ALU.add)
        nc.vector.scalar_tensor_tensor(
            out=late[:], in0=late[:], scalar=-0.5, in1=log_det[:, EARLIER:CLUSTERS, :], op0=ALU.mult, op1=ALU.subtract
        )

        z = keep.tile([P, ROW_TILES, CLUSTERS], F32)
        for first, last, energy in ((0, EARLIER, early), (EARLIER, CLUSTERS, late)):
            nc.vector.tensor_tensor(
                out=z[:, :, first:last],
                in0=energy[:].rearrange("p k j -> p j k"),
                in1=logits[:, first:last].unsqueeze(1).to_broadcast([P, ROW_TILES, last - first]),
                op=ALU.add,
            )
        z_max = keep.tile([P, ROW_TILES], F32)
        nc.vector.tensor_reduce(out=z_max[:], in_=z[:], axis=AXIS_X, op=ALU.max)
        nc.vector.tensor_tensor(
            out=z[:], in0=z[:], in1=z_max[:].unsqueeze(2).to_broadcast([P, ROW_TILES, CLUSTERS]), op=ALU.subtract
        )
        weight = keep.tile([P, ROW_TILES, CLUSTERS], F32)
        nc.scalar.activation(out=weight[:], in_=z[:], func=ACT.Exp)
        total = keep.tile([P, ROW_TILES], F32)
        nc.vector.tensor_reduce(out=total[:], in_=weight[:], axis=AXIS_X, op=ALU.add)
        nc.scalar.activation(out=total[:], in_=total[:], func=ACT.Ln)
        nc.vector.tensor_tensor(
            out=z[:], in0=z[:], in1=total[:].unsqueeze(2).to_broadcast([P, ROW_TILES, CLUSTERS]), op=ALU.subtract
        )
        nc.sync.dma_start(out=out_2.rearrange("(p j) k -> p j k", j=ROW_TILES), in_=z[:])
